import numpy as np
import ml_dtypes


def mxq(x, axis, fmt="e4m3"):
    dtype, down = {"e4m3": (ml_dtypes.float8_e4m3fn, 7), "e5m2": (ml_dtypes.float8_e5m2, 14)}[fmt]
    v = np.moveaxis(np.asarray(x, np.float32).astype(ml_dtypes.bfloat16).astype(np.float64), axis, -1)
    blocks = v.reshape(v.shape[:-1] + (-1, 32))
    amax = np.abs(blocks).max(-1, keepdims=True)
    byte = np.maximum(np.where(amax > 0, np.frexp(amax)[1] - 1 + 127, 0) - down, 1)
    scale = np.exp2(byte - 127.0)
    codes = (blocks / scale).astype(np.float32).astype(dtype).astype(np.float64)
    return np.moveaxis((codes * scale).reshape(v.shape), -1, axis)


WIDE = False


def mx_kscale(k):
    if not WIDE:
        return np.ones(k)
    levels = np.array([10, -10, 5, -5, 0])
    a = np.random.permutation(np.resize(levels, k // 512 * 4)).reshape(k // 512, 4)
    idx = np.arange(k)
    return np.exp2(a[idx // 512, idx % 128 // 32])


BF16 = ml_dtypes.bfloat16


def bf(x):
    return np.asarray(x, np.float32).astype(BF16)


def f64(x):
    return np.asarray(x).astype(np.float64)


B, S, T, U, F = 2, 512, 512, 512, 256
EPS = 1e-12


def setup_inputs():
    s = mx_kscale(T)
    return {"x1": bf(np.random.standard_normal((B, S, T)) * s),
            "x2": bf(np.random.standard_normal((B, S, F))),
            "W_query": bf(np.random.standard_normal((T, U)) * 0.7 / np.sqrt(T) / s[:, None]),
            "W_key": bf(np.random.standard_normal((F, U)) * 0.7 / np.sqrt(F)),
            "W_value": bf(np.random.standard_normal((U, T)) * 0.25 * np.sqrt(U))}


def reference(x1, x2, W_query, W_key, W_value):
    x1 = f64(x1)
    scores = (mxq(x1, 2, "e4m3") @ mxq(f64(W_query), 0, "e4m3")) + f64(x2) @ f64(W_key)
    t = np.tanh(scores)
    e = np.exp(t - t.max(-1, keepdims=True))
    a = e / e.sum(-1, keepdims=True)
    g = mxq(a, 2, "e4m3") @ mxq(f64(W_value), 0, "e4m3")
    out = g * x1
    sq = np.sum(out * out, axis=1, keepdims=True)
    return out * (1.0 / np.sqrt(np.maximum(sq, EPS)))

@@ -1,0 +1,226 @@
+from contextlib import ExitStack
+
+import concourse.mybir as mybir
+from concourse.masks import make_identity
+
+F32 = mybir.dt.float32
+BF16 = mybir.dt.bfloat16
+U32 = mybir.dt.uint32
+U8 = mybir.dt.uint8
+FP8X4 = mybir.dt.float8_e4m3fn_x4
+ACT = mybir.ActivationFunctionType
+ALU = mybir.AluOpType
+
+P = 128
+B, S, T, U, F = 2, 512, 512, 512, 256
+NI = S // P
+EPS = 1e-12
+
+FLOPS = 2 * B * S * T * U + 2 * B * S * F * U + 2 * B * S * U * T
+
+
+def tile_attentionlayer_pa_kernel(tc, x1, x2, W_query, W_key, W_value, out):
+    nc = tc.nc
+    with ExitStack() as ctx:
+        keep = ctx.enter_context(tc.tile_pool(name="keep", bufs=1))
+        work = ctx.enter_context(tc.tile_pool(name="work", bufs=3))
+        small = ctx.enter_context(tc.tile_pool(name="small", bufs=4))
+        psum = ctx.enter_context(tc.psum_pool(name="psum", bufs=1))
+
+        ident_f = keep.tile([P, P], F32, name="ident_f")
+        make_identity(nc, ident_f[:])
+        ident_b = keep.tile([P, P], BF16, name="ident_b")
+        make_identity(nc, ident_b[:])
+        neg_one = keep.tile([P, 1], F32, name="neg_one")
+        nc.vector.memset(neg_one[:], -1.0)
+        neg_half = keep.tile([P, 1], F32, name="neg_half")
+        nc.vector.memset(neg_half[:], -0.5)
+
+        x1n = [keep.tile([P, NI, T], BF16, name="x1n%d" % b) for b in range(B)]
+        x2n = [keep.tile([P, NI, F], BF16, name="x2n%d" % b) for b in range(B)]
+        wqr = keep.tile([P, 4, U], BF16, name="wqr")
+        wk = keep.tile([P, 2, U], BF16, name="wk")
+        wvr = keep.tile([P, 4, T], BF16, name="wvr")
+        x1v = [x1[b].rearrange("(p i) t -> p i t", i=NI) for b in range(B)]
+        x2v = [x2[b].rearrange("(p i) f -> p i f", i=NI) for b in range(B)]
+        nc.sync.dma_start(out=x1n[0][:, 0:2, :], in_=x1v[0][:, 0:2, :])
+        nc.sync.dma_start(out=x1n[0][:, 2:4, :], in_=x1v[0][:, 2:4, :])
+        nc.sync.dma_start(
+            out=wqr[:].rearrange("q (u e) c -> q u e c", u=2),
+            in_=W_query.rearrange("(u q e) c -> q u e c", u=2, e=2),
+        )
+        nc.sync.dma_start(out=x2n[0][:], in_=x2v[0])
+        nc.sync.dma_start(out=wk[:], in_=W_key.rearrange("(q e) c -> q e c", e=2))
+        nc.sync.dma_start(out=x1n[1][:], in_=x1v[1])
+        nc.sync.dma_start(out=x2n[1][:], in_=x2v[1])
+        nc.sync.dma_start(out=wvr[:], in_=W_value.rearrange("(j p) c -> p j c", p=P))
+
+        x1g = [keep.tile([P, 4 * S], BF16, name="x1g%d" % b, align_bytes=64) for b in range(B)]
+        x1c = [keep.tile([P, S], U32, name="x1c%d" % b, align_bytes=64) for b in range(B)]
+        x1s = [keep.tile([P, S], U8, name="x1s%d" % b, align_bytes=64) for b in range(B)]
+        x2t = [keep.tile([P, S], F32, name="x2t%d" % b) for b in range(B)]
+        ag = [keep.tile([P, 4 * S], BF16, name="ag%d" % b, align_bytes=64) for b in range(B)]
+        ac = [keep.tile([P, S], U32, name="ac%d" % b, align_bytes=64) for b in range(B)]
+        asc = [keep.tile([P, S], U8, name="asc%d" % b, align_bytes=64) for b in range(B)]
+        wqg = keep.tile([P, 4 * U], BF16, name="wqg", align_bytes=64)
+        wqc = keep.tile([P, U], U32, name="wqc", align_bytes=64)
+        wqs = keep.tile([P, U], U8, name="wqs", align_bytes=64)
+        wvg = keep.tile([P, 4 * T], BF16, name="wvg", align_bytes=64)
+        wvc = keep.tile([P, T], U32, name="wvc", align_bytes=64)
+        wvs = keep.tile([P, T], U8, name="wvs", align_bytes=64)
+        osb = [keep.tile([P, NI, T], F32, name="osb%d" % b) for b in range(B)]
+
+        def prep_x1(b, h):
+            x1w = x1n[b][:].bitcast(F32)
+            tin = psum.tile([P, 4, P], F32, name="tin", tag="tr", bufs=2)
+            for i2 in range(2):
+                for u in range(2):
+                    nc.tensor.transpose(
+                        tin[:, 2 * i2 + u, :], x1w[:, 2 * h + i2, P * u : P * u + P], ident_f[:]
+                    )
+            dst = x1g[b][:].bitcast(F32)[:, 512 * h : 512 * h + 512]
+            nc.scalar.copy(
+                out=dst.rearrange("p (i s u) -> p i s u", i=2, u=2),
+                in_=tin[:].rearrange("p (i u) s -> p i s u", u=2),
+            )
+            nc.vector.quantize_mx(
+                out=x1c[b][:, 256 * h : 256 * h + 256].bitcast(FP8X4),
+                scales=x1s[b][:, 256 * h : 256 * h + 256],
+                in_=x1g[b][:, 1024 * h : 1024 * h + 1024],
+            )
+
+        def prep_x2(b):
+            x2w = x2n[b][:].bitcast(F32)
+            tin = psum.tile([P, 4, P], F32, name="tin", tag="tr", bufs=2)
+            for i in range(NI):
+                nc.tensor.transpose(tin[:, i, :], x2w[:, i, :], ident_f[:])
+            nc.scalar.copy(out=x2t[b][:], in_=tin[:].rearrange("p i s -> p (i s)"))
+
+        def prep_wq():
+            nc.vector.tensor_copy(
+                out=wqg[:].rearrange("p (c i t) -> p c t i", i=4, t=4),
+                in_=wqr[:].rearrange("p t (c i) -> p c t i", i=4),
+            )
+            nc.vector.quantize_mx(out=wqc[:].bitcast(FP8X4), scales=wqs[:], in_=wqg[:])
+
+        def prep_wv():
+            for u in range(2):
+                nc.vector.tensor_copy(
+                    out=wvg[:, 1024 * u : 1024 * u + 1024].rearrange("p (e q j) -> p e q j", e=2, j=4),
+                    in_=wvr[:, :, 256 * u : 256 * u + 256].rearrange("p j (q e) -> p e q j", e=2),
+                )
+            nc.vector.quantize_mx(out=wvc[:].bitcast(FP8X4), scales=wvs[:], in_=wvg[:])
+
+        def stage1(b, i):
+            cols = slice(P * i, P * i + P)
+            sm = psum.tile([P, U], F32, name="sm", tag="sm", bufs=2)
+            nc.tensor.matmul_mx(
+                out=sm[:],
+                lhsT=x1c[b][:, cols].bitcast(FP8X4),
+                lhsT_scale=x1s[b][:, cols],
+                rhs=wqc[:].bitcast(FP8X4),
+                rhs_scale=wqs[:],
+                start=True,
+                stop=True,
+            )
+            sp = psum.tile([P, U], F32, name="sp", tag="sp", bufs=1)
+            x2b = x2t[b][:].bitcast(BF16).rearrange("p (s e) -> p s e", e=2)
+            for e in range(2):
+                nc.tensor.matmul(
+                    sp[:], lhsT=x2b[:, cols, e], rhs=wk[:, e, :], start=(e == 0), stop=(e == 1)
+                )
+            psb = work.tile([P, U], F32, name="psb")
+            nc.scalar.copy(out=psb[:], in_=sp[:])
+            sc = work.tile([P, U], F32, name="sc")
+            nc.vector.tensor_tensor(out=sc[:], in0=sm[:], in1=psb[:], op=ALU.add)
+            th = work.tile([P, U], F32, name="th")
+            nc.scalar.activation(out=th[:], in_=sc[:], func=ACT.Tanh)
+            ex = work.tile([P, U], F32, name="ex")
+            ssum = small.tile([P, 1], F32, name="ssum")
+            nc.scalar.activation(
+                out=ex[:], in_=th[:], func=ACT.Exp, bias=neg_one[:], accum_out=ssum[:]
+            )
+            rinv = small.tile([P, 1], F32, name="rinv")
+            nc.vector.reciprocal(out=rinv[:], in_=ssum[:])
+            a = work.tile([P, U], BF16, name="a")
+            nc.vector.tensor_scalar(
+                out=a[:], in0=ex[:], scalar1=rinv[:], scalar2=None, op0=ALU.mult
+            )
+            at = psum.tile([P, 4, P], BF16, name="at", tag="at", bufs=1)
+            for t in range(4):
+                nc.tensor.transpose(at[:, t, :], a[:, P * t : P * t + P], ident_b[:])
+            nc.vector.tensor_copy(
+                out=ag[b][:, 512 * i : 512 * i + 512].rearrange("p (s t) -> p s t", t=4),
+                in_=at[:].rearrange("p t s -> p s t"),
+            )
+            nc.vector.quantize_mx(
+                out=ac[b][:, cols].bitcast(FP8X4),
+                scales=asc[b][:, cols],
+                in_=ag[b][:, 512 * i : 512 * i + 512],
+            )
+
+        def stage2_chunk(b, c):
+            cols = slice(P * c, P * c + P)
+            g = psum.tile([P, S], F32, name="g", tag="g", bufs=2)
+            nc.tensor.matmul_mx(
+                out=g[:],
+                lhsT=wvc[:, cols].bitcast(FP8X4),
+                lhsT_scale=wvs[:, cols],
+                rhs=ac[b][:].bitcast(FP8X4),
+                rhs_scale=asc[b][:],
+                start=True,
+                stop=True,
+            )
+            y = work.tile([P, S], F32, name="y", bufs=4)
+            x1f = x1g[b][:].rearrange("p (s t) -> p s t", t=4)
+            nc.vector.tensor_tensor(out=y[:], in0=g[:], in1=x1f[:, :, c], op=ALU.mult)
+            junk = work.tile([P, S], BF16, name="junk", bufs=2)
+            q = small.tile([P, 1], F32, name="q")
+            nc.scalar.activation(out=junk[:], in_=y[:], func=ACT.Square, accum_out=q[:])
+            qm = small.tile([P, 1], F32, name="qm")
+            nc.gpsimd.tensor_scalar(out=qm[:], in0=q[:], scalar1=EPS, scalar2=None, op0=ALU.max)
+            rs = small.tile([P, 1], F32, name="rs")
+            nc.gpsimd.tensor_tensor(out=rs[:], in0=qm[:], in1=neg_half[:], op=ALU.pow)
+            ys = work.tile([P, S], F32, name="ys", bufs=4)
+            nc.vector.tensor_scalar(out=ys[:], in0=y[:], scalar1=rs[:], scalar2=None, op0=ALU.mult)
+            return ys
+
+        def stage2_pair(b, u):
+            ys = [stage2_chunk(b, 2 * u + e) for e in range(2)]
+            for h in range(2):
+                ot = psum.tile([P, 4, P], F32, name="ot", tag="tr", bufs=2)
+                for i2 in range(2):
+                    for e in range(2):
+                        si = P * (2 * h + i2)
+                        nc.tensor.transpose(ot[:, 2 * i2 + e, :], ys[e][:, si : si + P], ident_f[:])
+                nc.scalar.copy(
+                    out=osb[b][:, 2 * h : 2 * h + 2, 256 * u : 256 * u + 256].rearrange(
+                        "p i (q e) -> p i q e", e=2
+                    ),
+                    in_=ot[:].rearrange("p (i e) q -> p i q e", e=2),
+                )
+            nc.sync.dma_start(
+                out=out[b].rearrange("(p i) t -> p i t", i=NI)[:, :, 256 * u : 256 * u + 256],
+                in_=osb[b][:, :, 256 * u : 256 * u + 256],
+            )
+
+        prep_x1(0, 0)
+        prep_wq()
+        prep_x1(0, 1)
+        prep_x2(0)
+        stage1(0, 0)
+        stage1(0, 1)
+        prep_x1(1, 0)
+        stage1(0, 2)
+        prep_x1(1, 1)
+        prep_x2(1)
+        stage1(0, 3)
+        prep_wv()
+        stage1(1, 0)
+        stage2_pair(0, 0)
+        stage1(1, 1)
+        stage2_pair(0, 1)
+        stage1(1, 2)
+        stage1(1, 3)
+        stage2_pair(1, 0)
+        stage2_pair(1, 1)

@@ -19,6 +19,8 @@ EPS = 1e-12
 FLOPS = 2 * B * S * T * U + 2 * B * S * F * U + 2 * B * S * U * T
 
 
+TR_BUFS, ACC_BUFS, SP_BUFS, AT_BUFS = 2, 3, 2, 1
+
 def tile_attentionlayer_pa_kernel(tc, x1, x2, W_query, W_key, W_value, out):
     nc = tc.nc
     with ExitStack() as ctx:
@@ -26,6 +28,7 @@ def tile_attentionlayer_pa_kernel(tc, x1, x2, W_query, W_key, W_value, out):
         work = ctx.enter_context(tc.tile_pool(name="work", bufs=3))
         small = ctx.enter_context(tc.tile_pool(name="small", bufs=4))
         psum = ctx.enter_context(tc.psum_pool(name="psum", bufs=1))
+        ctx.enter_context(tc.manual_schedule())
 
         ident_f = keep.tile([P, P], F32, name="ident_f")
         make_identity(nc, ident_f[:])
@@ -70,100 +73,149 @@ def tile_attentionlayer_pa_kernel(tc, x1, x2, W_query, W_key, W_value, out):
         wvs = keep.tile([P, T], U8, name="wvs", align_bytes=64)
         osb = [keep.tile([P, NI, T], F32, name="osb%d" % b) for b in range(B)]
 
-        def prep_x1(b, h):
+        sm_t, sp_t, psb_t, sc_t, th_t, ex_t, ss_t, a_t, at_t = {}, {}, {}, {}, {}, {}, {}, {}, {}
+        tin_t, g_t, y_t, q_t, rs_t, ys_t, ot_t = {}, {}, {}, {}, {}, {}, {}
+
+        def pe_tx1(b, h):
             x1w = x1n[b][:].bitcast(F32)
-            tin = psum.tile([P, 4, P], F32, name="tin", tag="tr", bufs=2)
+            tin = psum.tile([P, 4, P], F32, name="tin", tag="tr", bufs=TR_BUFS)
+            tin_t[("x1", b, h)] = tin
             for i2 in range(2):
                 for u in range(2):
                     nc.tensor.transpose(
                         tin[:, 2 * i2 + u, :], x1w[:, 2 * h + i2, P * u : P * u + P], ident_f[:]
                     )
+
+        def x1_exit(eng_copy, b, h):
             dst = x1g[b][:].bitcast(F32)[:, 512 * h : 512 * h + 512]
-            nc.scalar.copy(
+            eng_copy(
                 out=dst.rearrange("p (i s u) -> p i s u", i=2, u=2),
-                in_=tin[:].rearrange("p (i u) s -> p i s u", u=2),
+                in_=tin_t[("x1", b, h)][:].rearrange("p (i u) s -> p i s u", u=2),
             )
+
+        def v_qx1(b, h):
             nc.vector.quantize_mx(
                 out=x1c[b][:, 256 * h : 256 * h + 256].bitcast(FP8X4),
                 scales=x1s[b][:, 256 * h : 256 * h + 256],
                 in_=x1g[b][:, 1024 * h : 1024 * h + 1024],
             )
 
-        def prep_x2(b):
+        def pe_tx2(b):
             x2w = x2n[b][:].bitcast(F32)
-            tin = psum.tile([P, 4, P], F32, name="tin", tag="tr", bufs=2)
+            tin = psum.tile([P, 4, P], F32, name="tin", tag="tr", bufs=TR_BUFS)
+            tin_t[("x2", b)] = tin
             for i in range(NI):
                 nc.tensor.transpose(tin[:, i, :], x2w[:, i, :], ident_f[:])
-            nc.scalar.copy(out=x2t[b][:], in_=tin[:].rearrange("p i s -> p (i s)"))
 
-        def prep_wq():
-            nc.vector.tensor_copy(
-                out=wqg[:].rearrange("p (c i t) -> p c t i", i=4, t=4),
-                in_=wqr[:].rearrange("p t (c i) -> p c t i", i=4),
+        def x2_exit(eng_copy, b):
+            eng_copy(out=x2t[b][:], in_=tin_t[("x2", b)][:].rearrange("p i s -> p (i s)"))
+
+        def wq_regroup(eng_copy, c):
+            eng_copy(
+                out=wqg[:, 512 * c : 512 * c + 512].rearrange("p (c i t) -> p c t i", i=4, t=4),
+                in_=wqr[:, :, P * c : P * c + P].rearrange("p t (c i) -> p c t i", i=4),
             )
-            nc.vector.quantize_mx(out=wqc[:].bitcast(FP8X4), scales=wqs[:], in_=wqg[:])
 
-        def prep_wv():
-            for u in range(2):
-                nc.vector.tensor_copy(
-                    out=wvg[:, 1024 * u : 1024 * u + 1024].rearrange("p (e q j) -> p e q j", e=2, j=4),
-                    in_=wvr[:, :, 256 * u : 256 * u + 256].rearrange("p j (q e) -> p e q j", e=2),
-                )
+        def v_wq_quant(c):
+            cc = slice(P * c, P * c + P)
+            nc.vector.quantize_mx(
+                out=wqc[:, cc].bitcast(FP8X4), scales=wqs[:, cc], in_=wqg[:, 512 * c : 512 * c + 512]
+            )
+
+        def wv_regroup(eng_copy, u):
+            eng_copy(
+                out=wvg[:, 1024 * u : 1024 * u + 1024].rearrange("p (e q j) -> p e q j", e=2, j=4),
+                in_=wvr[:, :, 256 * u : 256 * u + 256].rearrange("p j (q e) -> p e q j", e=2),
+            )
+
+        def v_wv_quant():
             nc.vector.quantize_mx(out=wvc[:].bitcast(FP8X4), scales=wvs[:], in_=wvg[:])
 
-        def stage1(b, i):
-            cols = slice(P * i, P * i + P)
-            sm = psum.tile([P, U], F32, name="sm", tag="sm", bufs=2)
+        mt_ps, mt_sb = {}, {}
+
+        def pe_mt(b, c):
+            cc = slice(P * c, P * c + P)
+            mt_ps[(b, c)] = psum.tile([P, S], F32, name="acc", tag="acc", bufs=ACC_BUFS)
             nc.tensor.matmul_mx(
-                out=sm[:],
-                lhsT=x1c[b][:, cols].bitcast(FP8X4),
-                lhsT_scale=x1s[b][:, cols],
-                rhs=wqc[:].bitcast(FP8X4),
-                rhs_scale=wqs[:],
+                out=mt_ps[(b, c)][:],
+                lhsT=wqc[:, cc].bitcast(FP8X4),
+                lhsT_scale=wqs[:, cc],
+                rhs=x1c[b][:].bitcast(FP8X4),
+                rhs_scale=x1s[b][:],
                 start=True,
                 stop=True,
             )
-            sp = psum.tile([P, U], F32, name="sp", tag="sp", bufs=1)
+
+        def mtx(eng_copy, b, c):
+            mt_sb[(b, c)] = work.tile([P, S], F32, name="mt", bufs=8)
+            eng_copy(out=mt_sb[(b, c)][:], in_=mt_ps[(b, c)][:])
+
+        def pe_p(k):
+            b, i = divmod(k, NI)
+            cols = slice(P * i, P * i + P)
+            sp = psum.tile([P, U], F32, name="sp", tag="sp", bufs=SP_BUFS)
+            sc_t[k] = sp
             x2b = x2t[b][:].bitcast(BF16).rearrange("p (s e) -> p s e", e=2)
             for e in range(2):
                 nc.tensor.matmul(
-                    sp[:], lhsT=x2b[:, cols, e], rhs=wk[:, e, :], start=(e == 0), stop=(e == 1)
+                    sp[:], lhsT=x2b[:, cols, e], rhs=wk[:, e, :], start=(e == 0), stop=False
                 )
-            psb = work.tile([P, U], F32, name="psb")
-            nc.scalar.copy(out=psb[:], in_=sp[:])
-            sc = work.tile([P, U], F32, name="sc")
-            nc.vector.tensor_tensor(out=sc[:], in0=sm[:], in1=psb[:], op=ALU.add)
-            th = work.tile([P, U], F32, name="th")
-            nc.scalar.activation(out=th[:], in_=sc[:], func=ACT.Tanh)
-            ex = work.tile([P, U], F32, name="ex")
-            ssum = small.tile([P, 1], F32, name="ssum")
+            for c in range(4):
+                nc.tensor.matmul(
+                    sp[:, P * c : P * c + P],
+                    lhsT=mt_sb[(b, c)][:, cols],
+                    rhs=ident_f[:],
+                    is_transpose=True,
+                    start=False,
+                    stop=(c == 3),
+                )
+
+        def s_th(k):
+            th_t[k] = work.tile([P, U], F32, name="th")
+            nc.scalar.activation(out=th_t[k][:], in_=sc_t[k][:], func=ACT.Tanh)
+
+        def s_ex(k):
+            ex_t[k] = work.tile([P, U], F32, name="ex")
+            ss_t[k] = small.tile([P, 1], F32, name="ssum")
             nc.scalar.activation(
-                out=ex[:], in_=th[:], func=ACT.Exp, bias=neg_one[:], accum_out=ssum[:]
+                out=ex_t[k][:], in_=th_t[k][:], func=ACT.Exp, bias=neg_one[:], accum_out=ss_t[k][:]
             )
+
+        def v_norm(k):
             rinv = small.tile([P, 1], F32, name="rinv")
-            nc.vector.reciprocal(out=rinv[:], in_=ssum[:])
-            a = work.tile([P, U], BF16, name="a")
+            nc.vector.reciprocal(out=rinv[:], in_=ss_t[k][:])
+            a_t[k] = work.tile([P, U], BF16, name="a")
             nc.vector.tensor_scalar(
-                out=a[:], in0=ex[:], scalar1=rinv[:], scalar2=None, op0=ALU.mult
+                out=a_t[k][:], in0=ex_t[k][:], scalar1=rinv[:], scalar2=None, op0=ALU.mult
             )
-            at = psum.tile([P, 4, P], BF16, name="at", tag="at", bufs=1)
+
+        def pe_at(k):
+            at_t[k] = psum.tile([P, 4, P], BF16, name="at", tag="at", bufs=AT_BUFS)
             for t in range(4):
-                nc.tensor.transpose(at[:, t, :], a[:, P * t : P * t + P], ident_b[:])
+                nc.tensor.transpose(at_t[k][:, t, :], a_t[k][:, P * t : P * t + P], ident_b[:])
+
+        def v_atx(k):
+            b, i = divmod(k, NI)
             nc.vector.tensor_copy(
                 out=ag[b][:, 512 * i : 512 * i + 512].rearrange("p (s t) -> p s t", t=4),
-                in_=at[:].rearrange("p t s -> p s t"),
+                in_=at_t[k][:].rearrange("p t s -> p s t"),
             )
+
+        def v_qa(k):
+            b, i = divmod(k, NI)
+            cols = slice(P * i, P * i + P)
             nc.vector.quantize_mx(
                 out=ac[b][:, cols].bitcast(FP8X4),
                 scales=asc[b][:, cols],
                 in_=ag[b][:, 512 * i : 512 * i + 512],
             )
 
-        def stage2_chunk(b, c):
+        def pe_mx2(j):
+            b, c = divmod(j, 4)
             cols = slice(P * c, P * c + P)
-            g = psum.tile([P, S], F32, name="g", tag="g", bufs=2)
+            g_t[j] = psum.tile([P, S], F32, name="acc", tag="acc", bufs=ACC_BUFS)
             nc.tensor.matmul_mx(
-                out=g[:],
+                out=g_t[j][:],
                 lhsT=wvc[:, cols].bitcast(FP8X4),
                 lhsT_scale=wvs[:, cols],
                 rhs=ac[b][:].bitcast(FP8X4),
@@ -171,56 +223,214 @@ def tile_attentionlayer_pa_kernel(tc, x1, x2, W_query, W_key, W_value, out):
                 start=True,
                 stop=True,
             )
-            y = work.tile([P, S], F32, name="y", bufs=4)
-            x1f = x1g[b][:].rearrange("p (s t) -> p s t", t=4)
-            nc.vector.tensor_tensor(out=y[:], in0=g[:], in1=x1f[:, :, c], op=ALU.mult)
-            junk = work.tile([P, S], BF16, name="junk", bufs=2)
-            q = small.tile([P, 1], F32, name="q")
-            nc.scalar.activation(out=junk[:], in_=y[:], func=ACT.Square, accum_out=q[:])
-            qm = small.tile([P, 1], F32, name="qm")
-            nc.gpsimd.tensor_scalar(out=qm[:], in0=q[:], scalar1=EPS, scalar2=None, op0=ALU.max)
-            rs = small.tile([P, 1], F32, name="rs")
-            nc.gpsimd.tensor_tensor(out=rs[:], in0=qm[:], in1=neg_half[:], op=ALU.pow)
-            ys = work.tile([P, S], F32, name="ys", bufs=4)
-            nc.vector.tensor_scalar(out=ys[:], in0=y[:], scalar1=rs[:], scalar2=None, op0=ALU.mult)
-            return ys
 
-        def stage2_pair(b, u):
-            ys = [stage2_chunk(b, 2 * u + e) for e in range(2)]
-            for h in range(2):
-                ot = psum.tile([P, 4, P], F32, name="ot", tag="tr", bufs=2)
-                for i2 in range(2):
-                    for e in range(2):
-                        si = P * (2 * h + i2)
-                        nc.tensor.transpose(ot[:, 2 * i2 + e, :], ys[e][:, si : si + P], ident_f[:])
-                nc.scalar.copy(
-                    out=osb[b][:, 2 * h : 2 * h + 2, 256 * u : 256 * u + 256].rearrange(
-                        "p i (q e) -> p i q e", e=2
-                    ),
-                    in_=ot[:].rearrange("p (i e) q -> p i q e", e=2),
-                )
+        def v_y(j):
+            b, c = divmod(j, 4)
+            y_t[j] = work.tile([P, S], F32, name="y", bufs=8)
+            x1f = x1g[b][:].rearrange("p (s t) -> p s t", t=4)
+            nc.vector.tensor_tensor(out=y_t[j][:], in0=g_t[j][:], in1=x1f[:, :, c], op=ALU.mult)
+
+        def s_sq(j):
+            junk = work.tile([P, S], BF16, name="junk", bufs=2)
+            q_t[j] = small.tile([P, 1], F32, name="q")
+            nc.scalar.activation(out=junk[:], in_=y_t[j][:], func=ACT.Square, accum_out=q_t[j][:])
+
+        def g_rs(j):
+            qm = small.tile([P, 1], F32, name="qm")
+            nc.gpsimd.tensor_scalar(out=qm[:], in0=q_t[j][:], scalar1=EPS, scalar2=None, op0=ALU.max)
+            rs_t[j] = small.tile([P, 1], F32, name="rs")
+            nc.gpsimd.tensor_tensor(out=rs_t[j][:], in0=qm[:], in1=neg_half[:], op=ALU.pow)
+
+        def v_scale(j):
+            ys_t[j] = work.tile([P, S], F32, name="ys", bufs=8)
+            nc.vector.tensor_scalar(
+                out=ys_t[j][:], in0=y_t[j][:], scalar1=rs_t[j][:], scalar2=None, op0=ALU.mult
+            )
+
+        def pe_ot(r, h):
+            ot_t[(r, h)] = psum.tile([P, 4, P], F32, name="ot", tag="tr", bufs=TR_BUFS)
+            for i2 in range(2):
+                for e in range(2):
+                    si = P * (2 * h + i2)
+                    nc.tensor.transpose(
+                        ot_t[(r, h)][:, 2 * i2 + e, :], ys_t[2 * r + e][:, si : si + P], ident_f[:]
+                    )
+
+        def ox(eng_copy, r, h):
+            b, u = divmod(r, 2)
+            eng_copy(
+                out=osb[b][:, 2 * h : 2 * h + 2, 256 * u : 256 * u + 256].rearrange(
+                    "p i (q e) -> p i q e", e=2
+                ),
+                in_=ot_t[(r, h)][:].rearrange("p (i e) q -> p i q e", e=2),
+            )
+
+        def d_store(r):
+            b, u = divmod(r, 2)
             nc.sync.dma_start(
                 out=out[b].rearrange("(p i) t -> p i t", i=NI)[:, :, 256 * u : 256 * u + 256],
                 in_=osb[b][:, :, 256 * u : 256 * u + 256],
             )
 
-        prep_x1(0, 0)
-        prep_wq()
-        prep_x1(0, 1)
-        prep_x2(0)
-        stage1(0, 0)
-        stage1(0, 1)
-        prep_x1(1, 0)
-        stage1(0, 2)
-        prep_x1(1, 1)
-        prep_x2(1)
-        stage1(0, 3)
-        prep_wv()
-        stage1(1, 0)
-        stage2_pair(0, 0)
-        stage1(1, 1)
-        stage2_pair(0, 1)
-        stage1(1, 2)
-        stage1(1, 3)
-        stage2_pair(1, 0)
-        stage2_pair(1, 1)
+        s_copy = nc.scalar.copy
+        v_copy = nc.vector.tensor_copy
+        NK = B * NI
+        pe_tx1(0, 0)
+        pe_tx1(0, 1)
+        x1_exit(s_copy, 0, 0)
+        v_qx1(0, 0)
+        x1_exit(s_copy, 0, 1)
+        wq_regroup(v_copy, 1)
+        v_qx1(0, 1)
+        wq_regroup(s_copy, 0)
+        v_wq_quant(1)
+        pe_tx2(0)
+        v_wq_quant(0)
+        wq_regroup(s_copy, 3)
+        pe_mt(0, 1)
+        wq_regroup(v_copy, 2)
+        v_wq_quant(2)
+        pe_mt(0, 0)
+        v_wq_quant(3)
+        x2_exit(s_copy, 0)
+        pe_mt(0, 2)
+        mtx(v_copy, 0, 1)
+        pe_tx1(1, 0)
+        mtx(s_copy, 0, 0)
+        pe_tx1(1, 1)
+        mtx(v_copy, 0, 2)
+        pe_mt(0, 3)
+        x1_exit(s_copy, 1, 0)
+        x1_exit(v_copy, 1, 1)
+        pe_tx2(1)
+        v_qx1(1, 0)
+        mtx(s_copy, 0, 3)
+        v_qx1(1, 1)
+        pe_p(3)
+        x2_exit(s_copy, 1)
+        wv_regroup(v_copy, 1)
+        pe_mt(1, 1)
+        s_th(3)
+        pe_mt(1, 2)
+        wv_regroup(v_copy, 0)
+        pe_mt(1, 3)
+        v_wv_quant()
+        pe_p(1)
+        s_ex(3)
+        mtx(v_copy, 1, 2)
+        pe_p(2)
+        v_norm(3)
+        mtx(s_copy, 1, 1)
+        s_th(1)
+        mtx(v_copy, 1, 3)
+        pe_mt(1, 0)
+        s_ex(1)
+        pe_p(0)
+        s_th(2)
+        v_norm(1)
+        pe_at(3)
+        s_ex(2)
+        mtx(v_copy, 1, 0)
+        pe_p(5)
+        v_atx(3)
+        s_th(0)
+        v_norm(2)
+        s_ex(0)
+        pe_at(1)
+        pe_p(6)
+        v_qa(3)
+        v_atx(1)
+        s_th(5)
+        v_norm(0)
+        pe_at(2)
+        s_ex(5)
+        pe_p(7)
+        v_qa(1)
+        v_atx(2)
+        s_th(6)
+        v_norm(5)
+        pe_at(0)
+        s_ex(6)
+        pe_p(4)
+        v_qa(2)
+        v_atx(0)
+        s_th(7)
+        v_norm(6)
+        pe_at(5)
+        s_ex(7)
+        v_qa(0)
+        v_atx(5)
+        s_th(4)
+        pe_mx2(1)
+        v_norm(7)
+        pe_mx2(3)
+        s_ex(4)
+        pe_at(6)
+        v_y(1)
+        pe_mx2(0)
+        v_atx(6)
+        s_sq(1)
+        pe_mx2(2)
+        v_norm(4)
+        pe_at(7)
+        v_qa(6)
+        g_rs(1)
+        v_y(3)
+        v_atx(7)
+        s_sq(3)
+        v_y(2)
+        pe_at(4)
+        g_rs(3)
+        v_y(0)
+        s_sq(2)
+        v_atx(4)
+        s_sq(0)
+        g_rs(2)
+        v_qa(5)
+        v_qa(7)
+        v_qa(4)
+        v_scale(1)
+        g_rs(0)
+        pe_mx2(7)
+        v_scale(3)
+        v_scale(2)
+        pe_mx2(5)
+        pe_mx2(6)
+        v_y(7)
+        pe_ot(1, 0)
+        v_y(5)
+        pe_ot(1, 1)
+        s_sq(7)
+        pe_mx2(4)
+        v_y(6)
+        s_sq(5)
+        g_rs(7)
+        v_scale(0)
+        v_y(4)
+        s_sq(6)
+        g_rs(5)
+        v_scale(7)
+        s_sq(4)
+        ox(v_copy, 1, 0)
+        g_rs(6)
+        v_scale(5)
+        pe_ot(0, 1)
+        ox(s_copy, 1, 1)
+        pe_ot(0, 0)
+        d_store(1)
+        g_rs(4)
+        v_scale(6)
+        ox(s_copy, 0, 1)
+        ox(v_copy, 0, 0)
+        pe_ot(3, 0)
+        v_scale(4)
+        d_store(0)
+        pe_ot(3, 1)
+        ox(v_copy, 3, 0)
+        pe_ot(2, 1)
+        ox(s_copy, 3, 1)
+        pe_ot(2, 0)
+        d_store(3)
+        ox(s_copy, 2, 1)
+        ox(v_copy, 2, 0)
+        d_store(2)

@@ -19,7 +19,7 @@ EPS = 1e-12
 FLOPS = 2 * B * S * T * U + 2 * B * S * F * U + 2 * B * S * U * T
 
 
-TR_BUFS, ACC_BUFS, SP_BUFS, AT_BUFS = 2, 3, 2, 1
+TR_BUFS, ACC_BUFS, SP_BUFS, AT_BUFS = 2, 2, 2, 2
 
 def tile_attentionlayer_pa_kernel(tc, x1, x2, W_query, W_key, W_value, out):
     nc = tc.nc
@@ -47,13 +47,13 @@ def tile_attentionlayer_pa_kernel(tc, x1, x2, W_query, W_key, W_value, out):
         x1v = [x1[b].rearrange("(p i) t -> p i t", i=NI) for b in range(B)]
         x2v = [x2[b].rearrange("(p i) f -> p i f", i=NI) for b in range(B)]
         nc.sync.dma_start(out=x1n[0][:, 0:2, :], in_=x1v[0][:, 0:2, :])
-        nc.sync.dma_start(out=x1n[0][:, 2:4, :], in_=x1v[0][:, 2:4, :])
         nc.sync.dma_start(
             out=wqr[:].rearrange("q (u e) c -> q u e c", u=2),
             in_=W_query.rearrange("(u q e) c -> q u e c", u=2, e=2),
         )
         nc.sync.dma_start(out=x2n[0][:], in_=x2v[0])
         nc.sync.dma_start(out=wk[:], in_=W_key.rearrange("(q e) c -> q e c", e=2))
+        nc.sync.dma_start(out=x1n[0][:, 2:4, :], in_=x1v[0][:, 2:4, :])
         nc.sync.dma_start(out=x1n[1][:], in_=x1v[1])
         nc.sync.dma_start(out=x2n[1][:], in_=x2v[1])
         nc.sync.dma_start(out=wvr[:], in_=W_value.rearrange("(j p) c -> p j c", p=P))
@@ -74,7 +74,7 @@ def tile_attentionlayer_pa_kernel(tc, x1, x2, W_query, W_key, W_value, out):
         osb = [keep.tile([P, NI, T], F32, name="osb%d" % b) for b in range(B)]
 
         sm_t, sp_t, psb_t, sc_t, th_t, ex_t, ss_t, a_t, at_t = {}, {}, {}, {}, {}, {}, {}, {}, {}
-        tin_t, g_t, y_t, q_t, rs_t, ys_t, ot_t = {}, {}, {}, {}, {}, {}, {}
+        tin_t, g_t, y_t, q_t, rs_t, ys_t, ot_t, ri_t = {}, {}, {}, {}, {}, {}, {}, {}
 
         def pe_tx1(b, h):
             x1w = x1n[b][:].bitcast(F32)
@@ -133,24 +133,27 @@ def tile_attentionlayer_pa_kernel(tc, x1, x2, W_query, W_key, W_value, out):
 
         mt_ps, mt_sb = {}, {}
 
-        def pe_mt(b, c):
-            cc = slice(P * c, P * c + P)
-            mt_ps[(b, c)] = psum.tile([P, S], F32, name="acc", tag="acc", bufs=ACC_BUFS)
-            nc.tensor.matmul_mx(
-                out=mt_ps[(b, c)][:],
-                lhsT=wqc[:, cc].bitcast(FP8X4),
-                lhsT_scale=wqs[:, cc],
-                rhs=x1c[b][:].bitcast(FP8X4),
-                rhs_scale=x1s[b][:],
-                start=True,
-                stop=True,
-            )
+        def pe_mt(k):
+            b, i = divmod(k, NI)
+            cols = slice(P * i, P * i + P)
+            mt_ps[k] = psum.tile([P, 4, P], F32, name="acc", tag="acc", bufs=ACC_BUFS)
+            for c in range(4):
+                cc = slice(P * c, P * c + P)
+                nc.tensor.matmul_mx(
+                    out=mt_ps[k][:, c, :],
+                    lhsT=wqc[:, cc].bitcast(FP8X4),
+                    lhsT_scale=wqs[:, cc],
+                    rhs=x1c[b][:, cols].bitcast(FP8X4),
+                    rhs_scale=x1s[b][:, cols],
+                    start=True,
+                    stop=True,
+                )
 
-        def mtx(eng_copy, b, c):
-            mt_sb[(b, c)] = work.tile([P, S], F32, name="mt", bufs=8)
-            eng_copy(out=mt_sb[(b, c)][:], in_=mt_ps[(b, c)][:])
+        def mtx(eng_copy, k):
+            mt_sb[k] = work.tile([P, 4, P], F32, name="mt", bufs=3)
+            eng_copy(out=mt_sb[k][:], in_=mt_ps[k][:])
 
-        def pe_p(k):
+        def pe_pa(k):
             b, i = divmod(k, NI)
             cols = slice(P * i, P * i + P)
             sp = psum.tile([P, U], F32, name="sp", tag="sp", bufs=SP_BUFS)
@@ -160,10 +163,13 @@ def tile_attentionlayer_pa_kernel(tc, x1, x2, W_query, W_key, W_value, out):
                 nc.tensor.matmul(
                     sp[:], lhsT=x2b[:, cols, e], rhs=wk[:, e, :], start=(e == 0), stop=False
                 )
+
+        def pe_pb(k):
+            sp = sc_t[k]
             for c in range(4):
                 nc.tensor.matmul(
                     sp[:, P * c : P * c + P],
-                    lhsT=mt_sb[(b, c)][:, cols],
+                    lhsT=mt_sb[k][:, c, :],
                     rhs=ident_f[:],
                     is_transpose=True,
                     start=False,
@@ -181,22 +187,32 @@ def tile_attentionlayer_pa_kernel(tc, x1, x2, W_query, W_key, W_value, out):
                 out=ex_t[k][:], in_=th_t[k][:], func=ACT.Exp, bias=neg_one[:], accum_out=ss_t[k][:]
             )
 
-        def v_norm(k):
-            rinv = small.tile([P, 1], F32, name="rinv")
-            nc.vector.reciprocal(out=rinv[:], in_=ss_t[k][:])
+        def v_rinv(k):
+            ri_t[k] = small.tile([P, 1], F32, name="rinv")
+            nc.vector.reciprocal(out=ri_t[k][:], in_=ss_t[k][:])
+
+        def scale_rows(eng, dst, src, col):
+            if eng == "v":
+                nc.vector.tensor_scalar(out=dst, in0=src, scalar1=col, scalar2=None, op0=ALU.mult)
+            elif eng == "s":
+                nc.scalar.activation(out=dst, in_=src, func=ACT.Copy, scale=col)
+            else:
+                nc.gpsimd.tensor_scalar(
+                    out=dst, in0=src, scalar1=col, scalar2=0.0, op0=ALU.mult, op1=ALU.add
+                )
+
+        def norm(eng, k):
             a_t[k] = work.tile([P, U], BF16, name="a")
-            nc.vector.tensor_scalar(
-                out=a_t[k][:], in0=ex_t[k][:], scalar1=rinv[:], scalar2=None, op0=ALU.mult
-            )
+            scale_rows(eng, a_t[k][:], ex_t[k][:], ri_t[k][:])
 
         def pe_at(k):
             at_t[k] = psum.tile([P, 4, P], BF16, name="at", tag="at", bufs=AT_BUFS)
             for t in range(4):
                 nc.tensor.transpose(at_t[k][:, t, :], a_t[k][:, P * t : P * t + P], ident_b[:])
 
-        def v_atx(k):
+        def atx(eng_copy, k):
             b, i = divmod(k, NI)
-            nc.vector.tensor_copy(
+            eng_copy(
                 out=ag[b][:, 512 * i : 512 * i + 512].rearrange("p (s t) -> p s t", t=4),
                 in_=at_t[k][:].rearrange("p t s -> p s t"),
             )
@@ -241,11 +257,9 @@ def tile_attentionlayer_pa_kernel(tc, x1, x2, W_query, W_key, W_value, out):
             rs_t[j] = small.tile([P, 1], F32, name="rs")
             nc.gpsimd.tensor_tensor(out=rs_t[j][:], in0=qm[:], in1=neg_half[:], op=ALU.pow)
 
-        def v_scale(j):
+        def scale(eng, j):
             ys_t[j] = work.tile([P, S], F32, name="ys", bufs=8)
-            nc.vector.tensor_scalar(
-                out=ys_t[j][:], in0=y_t[j][:], scalar1=rs_t[j][:], scalar2=None, op0=ALU.mult
-            )
+            scale_rows(eng, ys_t[j][:], y_t[j][:], rs_t[j][:])
 
         def pe_ot(r, h):
             ot_t[(r, h)] = psum.tile([P, 4, P], F32, name="ot", tag="tr", bufs=TR_BUFS)
@@ -265,172 +279,194 @@ def tile_attentionlayer_pa_kernel(tc, x1, x2, W_query, W_key, W_value, out):
                 in_=ot_t[(r, h)][:].rearrange("p (i e) q -> p i q e", e=2),
             )
 
-        def d_store(r):
+        def d_store(r, h):
             b, u = divmod(r, 2)
             nc.sync.dma_start(
-                out=out[b].rearrange("(p i) t -> p i t", i=NI)[:, :, 256 * u : 256 * u + 256],
-                in_=osb[b][:, :, 256 * u : 256 * u + 256],
+                out=out[b].rearrange("(p i) t -> p i t", i=NI)[
+                    :, 2 * h : 2 * h + 2, 256 * u : 256 * u + 256
+                ],
+                in_=osb[b][:, 2 * h : 2 * h + 2, 256 * u : 256 * u + 256],
             )
 
         s_copy = nc.scalar.copy
         v_copy = nc.vector.tensor_copy
         NK = B * NI
+        wq_regroup(v_copy, 0)
+        wq_regroup(s_copy, 1)
         pe_tx1(0, 0)
-        pe_tx1(0, 1)
-        x1_exit(s_copy, 0, 0)
-        v_qx1(0, 0)
-        x1_exit(s_copy, 0, 1)
-        wq_regroup(v_copy, 1)
-        v_qx1(0, 1)
-        wq_regroup(s_copy, 0)
+        wq_regroup(v_copy, 3)
+        x1_exit(v_copy, 0, 0)
         v_wq_quant(1)
-        pe_tx2(0)
+        v_qx1(0, 0)
         v_wq_quant(0)
-        wq_regroup(s_copy, 3)
-        pe_mt(0, 1)
-        wq_regroup(v_copy, 2)
+        pe_tx2(0)
+        wq_regroup(s_copy, 2)
         v_wq_quant(2)
-        pe_mt(0, 0)
         v_wq_quant(3)
+        pe_tx1(0, 1)
+        x1_exit(v_copy, 0, 1)
+        pe_mt(0)
         x2_exit(s_copy, 0)
-        pe_mt(0, 2)
-        mtx(v_copy, 0, 1)
+        pe_pa(0)
+        mtx(v_copy, 0)
+        v_qx1(0, 1)
         pe_tx1(1, 0)
-        mtx(s_copy, 0, 0)
-        pe_tx1(1, 1)
-        mtx(v_copy, 0, 2)
-        pe_mt(0, 3)
-        x1_exit(s_copy, 1, 0)
-        x1_exit(v_copy, 1, 1)
-        pe_tx2(1)
+        x1_exit(v_copy, 1, 0)
+        pe_mt(1)
+        pe_pb(0)
         v_qx1(1, 0)
-        mtx(s_copy, 0, 3)
-        v_qx1(1, 1)
-        pe_p(3)
-        x2_exit(s_copy, 1)
-        wv_regroup(v_copy, 1)
-        pe_mt(1, 1)
-        s_th(3)
-        pe_mt(1, 2)
-        wv_regroup(v_copy, 0)
-        pe_mt(1, 3)
-        v_wv_quant()
-        pe_p(1)
-        s_ex(3)
-        mtx(v_copy, 1, 2)
-        pe_p(2)
-        v_norm(3)
-        mtx(s_copy, 1, 1)
-        s_th(1)
-        mtx(v_copy, 1, 3)
-        pe_mt(1, 0)
-        s_ex(1)
-        pe_p(0)
-        s_th(2)
-        v_norm(1)
-        pe_at(3)
-        s_ex(2)
-        mtx(v_copy, 1, 0)
-        pe_p(5)
-        v_atx(3)
+        wv_regroup(s_copy, 0)
+        mtx(v_copy, 1)
+        pe_mt(2)
+        pe_pa(1)
         s_th(0)
-        v_norm(2)
+        pe_tx2(1)
+        pe_pb(1)
+        mtx(s_copy, 2)
+        pe_mt(3)
+        pe_mt(5)
+        x2_exit(v_copy, 1)
         s_ex(0)
-        pe_at(1)
-        pe_p(6)
-        v_qa(3)
-        v_atx(1)
-        s_th(5)
-        v_norm(0)
-        pe_at(2)
-        s_ex(5)
-        pe_p(7)
-        v_qa(1)
-        v_atx(2)
-        s_th(6)
-        v_norm(5)
+        s_th(1)
+        pe_pa(2)
+        pe_pb(2)
+        s_ex(1)
+        mtx(v_copy, 3)
+        pe_tx1(1, 1)
+        s_th(2)
+        mtx(v_copy, 5)
+        v_rinv(0)
+        pe_pa(3)
+        pe_mt(4)
+        norm("v", 0)
+        v_rinv(1)
+        norm("v", 1)
+        pe_pb(3)
+        x1_exit(v_copy, 1, 1)
         pe_at(0)
+        v_qx1(1, 1)
+        s_ex(2)
+        mtx(s_copy, 4)
+        pe_at(1)
+        pe_pa(4)
+        pe_pb(4)
+        pe_mt(6)
+        s_th(3)
+        pe_pa(5)
+        v_rinv(2)
+        s_ex(3)
+        norm("v", 2)
+        wv_regroup(v_copy, 1)
+        atx(v_copy, 0)
+        v_rinv(3)
+        pe_mt(7)
+        pe_at(2)
+        s_th(4)
+        pe_pb(5)
+        atx(v_copy, 1)
+        mtx(s_copy, 6)
+        pe_pa(6)
+        s_ex(4)
+        s_th(5)
+        norm("v", 3)
+        v_wv_quant()
+        s_ex(5)
+        pe_at(3)
+        pe_pb(6)
+        s_th(6)
+        mtx(v_copy, 7)
+        v_qa(1)
         s_ex(6)
-        pe_p(4)
-        v_qa(2)
-        v_atx(0)
+        v_rinv(4)
+        atx(v_copy, 3)
+        pe_pa(7)
+        atx(v_copy, 2)
+        v_rinv(5)
+        v_qa(0)
+        pe_pb(7)
+        norm("v", 5)
         s_th(7)
-        v_norm(6)
+        norm("v", 4)
+        v_qa(3)
         pe_at(5)
         s_ex(7)
-        v_qa(0)
-        v_atx(5)
-        s_th(4)
-        pe_mx2(1)
-        v_norm(7)
-        pe_mx2(3)
-        s_ex(4)
-        pe_at(6)
-        v_y(1)
+        v_qa(2)
+        v_rinv(6)
+        pe_at(4)
         pe_mx2(0)
-        v_atx(6)
-        s_sq(1)
-        pe_mx2(2)
-        v_norm(4)
+        atx(v_copy, 5)
+        norm("s", 6)
+        v_rinv(7)
+        v_y(0)
+        norm("s", 7)
+        atx(v_copy, 4)
+        pe_mx2(1)
+        s_sq(0)
+        pe_at(6)
+        v_qa(5)
+        v_y(1)
         pe_at(7)
+        atx(s_copy, 6)
+        g_rs(0)
+        s_sq(1)
+        v_qa(4)
+        atx(v_copy, 7)
+        pe_mx2(2)
         v_qa(6)
         g_rs(1)
-        v_y(3)
-        v_atx(7)
-        s_sq(3)
         v_y(2)
-        pe_at(4)
-        g_rs(3)
-        v_y(0)
-        s_sq(2)
-        v_atx(4)
-        s_sq(0)
-        g_rs(2)
-        v_qa(5)
         v_qa(7)
-        v_qa(4)
-        v_scale(1)
-        g_rs(0)
-        pe_mx2(7)
-        v_scale(3)
-        v_scale(2)
+        pe_mx2(3)
+        v_y(3)
+        scale("v", 1)
+        scale("s", 0)
+        s_sq(2)
+        pe_mx2(4)
+        g_rs(2)
         pe_mx2(5)
+        s_sq(3)
+        v_y(4)
+        pe_ot(0, 1)
+        g_rs(3)
+        s_sq(4)
+        g_rs(4)
+        v_y(5)
         pe_mx2(6)
+        scale("v", 2)
+        ox(v_copy, 0, 1)
+        scale("v", 3)
+        pe_ot(0, 0)
+        v_y(6)
+        pe_mx2(7)
+        s_sq(5)
+        ox(s_copy, 0, 0)
+        s_sq(6)
         v_y(7)
         pe_ot(1, 0)
-        v_y(5)
-        pe_ot(1, 1)
-        s_sq(7)
-        pe_mx2(4)
-        v_y(6)
-        s_sq(5)
-        g_rs(7)
-        v_scale(0)
-        v_y(4)
-        s_sq(6)
         g_rs(5)
-        v_scale(7)
-        s_sq(4)
+        s_sq(7)
+        scale("v", 4)
         ox(v_copy, 1, 0)
-        g_rs(6)
-        v_scale(5)
-        pe_ot(0, 1)
+        pe_ot(1, 1)
         ox(s_copy, 1, 1)
-        pe_ot(0, 0)
-        d_store(1)
-        g_rs(4)
-        v_scale(6)
-        ox(s_copy, 0, 1)
-        ox(v_copy, 0, 0)
-        pe_ot(3, 0)
-        v_scale(4)
-        d_store(0)
-        pe_ot(3, 1)
-        ox(v_copy, 3, 0)
-        pe_ot(2, 1)
-        ox(s_copy, 3, 1)
+        g_rs(6)
+        g_rs(7)
+        scale("v", 5)
+        d_store(1, 1)
         pe_ot(2, 0)
-        d_store(3)
-        ox(s_copy, 2, 1)
+        d_store(0, 1)
         ox(v_copy, 2, 0)
-        d_store(2)
+        scale("s", 6)
+        scale("v", 7)
+        d_store(1, 0)
+        d_store(0, 0)
+        pe_ot(2, 1)
+        ox(s_copy, 2, 1)
+        d_store(2, 1)
+        pe_ot(3, 0)
+        d_store(2, 0)
+        pe_ot(3, 1)
+        ox(s_copy, 3, 1)
+        ox(v_copy, 3, 0)
+        d_store(3, 0)
+        d_store(3, 1)

@@ -71,7 +71,10 @@ def tile_attentionlayer_pa_kernel(tc, x1, x2, W_query, W_key, W_value, out):
         wvg = keep.tile([P, 4 * T], BF16, name="wvg", align_bytes=64)
         wvc = keep.tile([P, T], U32, name="wvc", align_bytes=64)
         wvs = keep.tile([P, T], U8, name="wvs", align_bytes=64)
-        osb = [keep.tile([P, NI, T], F32, name="osb%d" % b) for b in range(B)]
+        osb = {}
+        for r in range(2 * B):
+            for h in range(2):
+                osb[(r, h)] = keep.tile([P, 2, 256], F32, name="osb%d%d" % (r, h))
 
         sm_t, sp_t, psb_t, sc_t, th_t, ex_t, ss_t, a_t, at_t = {}, {}, {}, {}, {}, {}, {}, {}, {}
         tin_t, g_t, y_t, q_t, rs_t, ys_t, ot_t, ri_t = {}, {}, {}, {}, {}, {}, {}, {}
@@ -271,11 +274,8 @@ def tile_attentionlayer_pa_kernel(tc, x1, x2, W_query, W_key, W_value, out):
                     )
 
         def ox(eng_copy, r, h):
-            b, u = divmod(r, 2)
             eng_copy(
-                out=osb[b][:, 2 * h : 2 * h + 2, 256 * u : 256 * u + 256].rearrange(
-                    "p i (q e) -> p i q e", e=2
-                ),
+                out=osb[(r, h)][:].rearrange("p i (q e) -> p i q e", e=2),
                 in_=ot_t[(r, h)][:].rearrange("p (i e) q -> p i q e", e=2),
             )
 
@@ -285,7 +285,7 @@ def tile_attentionlayer_pa_kernel(tc, x1, x2, W_query, W_key, W_value, out):
                 out=out[b].rearrange("(p i) t -> p i t", i=NI)[
                     :, 2 * h : 2 * h + 2, 256 * u : 256 * u + 256
                 ],
-                in_=osb[b][:, 2 * h : 2 * h + 2, 256 * u : 256 * u + 256],
+                in_=osb[(r, h)][:],
             )
 
         s_copy = nc.scalar.copy
@@ -434,12 +434,14 @@ def tile_attentionlayer_pa_kernel(tc, x1, x2, W_query, W_key, W_value, out):
         pe_mx2(6)
         scale("v", 2)
         ox(v_copy, 0, 1)
+        d_store(0, 1)
         scale("v", 3)
         pe_ot(0, 0)
         v_y(6)
         pe_mx2(7)
         s_sq(5)
         ox(s_copy, 0, 0)
+        d_store(0, 0)
         s_sq(6)
         v_y(7)
         pe_ot(1, 0)
@@ -447,26 +449,24 @@ def tile_attentionlayer_pa_kernel(tc, x1, x2, W_query, W_key, W_value, out):
         s_sq(7)
         scale("v", 4)
         ox(v_copy, 1, 0)
+        d_store(1, 0)
         pe_ot(1, 1)
         ox(s_copy, 1, 1)
+        d_store(1, 1)
         g_rs(6)
         g_rs(7)
         scale("v", 5)
-        d_store(1, 1)
         pe_ot(2, 0)
-        d_store(0, 1)
         ox(v_copy, 2, 0)
+        d_store(2, 0)
         scale("s", 6)
         scale("v", 7)
-        d_store(1, 0)
-        d_store(0, 0)
         pe_ot(2, 1)
         ox(s_copy, 2, 1)
         d_store(2, 1)
         pe_ot(3, 0)
-        d_store(2, 0)
         pe_ot(3, 1)
         ox(s_copy, 3, 1)
+        d_store(3, 1)
         ox(v_copy, 3, 0)
         d_store(3, 0)
-        d_store(3, 1)

@@ -19,7 +19,7 @@ EPS = 1e-12
 FLOPS = 2 * B * S * T * U + 2 * B * S * F * U + 2 * B * S * U * T
 
 
-TR_BUFS, ACC_BUFS, SP_BUFS, AT_BUFS = 2, 2, 2, 2
+TR_BUFS, ACC_BUFS, SP_BUFS = 4, 2, 2
 
 def tile_attentionlayer_pa_kernel(tc, x1, x2, W_query, W_key, W_value, out):
     nc = tc.nc
@@ -32,8 +32,6 @@ def tile_attentionlayer_pa_kernel(tc, x1, x2, W_query, W_key, W_value, out):
 
         ident_f = keep.tile([P, P], F32, name="ident_f")
         make_identity(nc, ident_f[:])
-        ident_b = keep.tile([P, P], BF16, name="ident_b")
-        make_identity(nc, ident_b[:])
         neg_one = keep.tile([P, 1], F32, name="neg_one")
         nc.vector.memset(neg_one[:], -1.0)
         neg_half = keep.tile([P, 1], F32, name="neg_half")
@@ -51,12 +49,15 @@ def tile_attentionlayer_pa_kernel(tc, x1, x2, W_query, W_key, W_value, out):
             out=wqr[:].rearrange("q (u e) c -> q u e c", u=2),
             in_=W_query.rearrange("(u q e) c -> q u e c", u=2, e=2),
         )
+        nc.sync.dma_start(out=x1n[0][:, 2:4, :], in_=x1v[0][:, 2:4, :])
         nc.sync.dma_start(out=x2n[0][:], in_=x2v[0])
         nc.sync.dma_start(out=wk[:], in_=W_key.rearrange("(q e) c -> q e c", e=2))
-        nc.sync.dma_start(out=x1n[0][:, 2:4, :], in_=x1v[0][:, 2:4, :])
         nc.sync.dma_start(out=x1n[1][:], in_=x1v[1])
         nc.sync.dma_start(out=x2n[1][:], in_=x2v[1])
-        nc.sync.dma_start(out=wvr[:], in_=W_value.rearrange("(j p) c -> p j c", p=P))
+        nc.sync.dma_start(
+            out=wvr[:].rearrange("q (u e) c -> q u e c", u=2),
+            in_=W_value.rearrange("(u q e) c -> q u e c", u=2, e=2),
+        )
 
         x1g = [keep.tile([P, 4 * S], BF16, name="x1g%d" % b, align_bytes=64) for b in range(B)]
         x1c = [keep.tile([P, S], U32, name="x1c%d" % b, align_bytes=64) for b in range(B)]
@@ -134,6 +135,9 @@ def tile_attentionlayer_pa_kernel(tc, x1, x2, W_query, W_key, W_value, out):
         def v_wv_quant():
             nc.vector.quantize_mx(out=wvc[:].bitcast(FP8X4), scales=wvs[:], in_=wvg[:])
 
+        def g_copy(out, in_):
+            nc.gpsimd.tensor_scalar(out=out, in0=in_, scalar1=1.0, scalar2=0.0, op0=ALU.mult, op1=ALU.add)
+
         mt_ps, mt_sb = {}, {}
 
         def pe_mt(k):
@@ -209,15 +213,16 @@ def tile_attentionlayer_pa_kernel(tc, x1, x2, W_query, W_key, W_value, out):
             scale_rows(eng, a_t[k][:], ex_t[k][:], ri_t[k][:])
 
         def pe_at(k):
-            at_t[k] = psum.tile([P, 4, P], BF16, name="at", tag="at", bufs=AT_BUFS)
-            for t in range(4):
-                nc.tensor.transpose(at_t[k][:, t, :], a_t[k][:, P * t : P * t + P], ident_b[:])
+            at_t[k] = psum.tile([P, 2, P], F32, name="at", tag="tr", bufs=TR_BUFS)
+            a_words = a_t[k][:].bitcast(F32)
+            for u in range(2):
+                nc.tensor.transpose(at_t[k][:, u, :], a_words[:, P * u : P * u + P], ident_f[:])
 
         def atx(eng_copy, k):
             b, i = divmod(k, NI)
             eng_copy(
-                out=ag[b][:, 512 * i : 512 * i + 512].rearrange("p (s t) -> p s t", t=4),
-                in_=at_t[k][:].rearrange("p t s -> p s t"),
+                out=ag[b][:].bitcast(F32)[:, 256 * i : 256 * i + 256].rearrange("p (s u) -> p s u", u=2),
+                in_=at_t[k][:].rearrange("p u s -> p s u"),
             )
 
         def v_qa(k):
@@ -291,182 +296,145 @@ def tile_attentionlayer_pa_kernel(tc, x1, x2, W_query, W_key, W_value, out):
         s_copy = nc.scalar.copy
         v_copy = nc.vector.tensor_copy
         NK = B * NI
-        wq_regroup(v_copy, 0)
-        wq_regroup(s_copy, 1)
+
         pe_tx1(0, 0)
-        wq_regroup(v_copy, 3)
         x1_exit(v_copy, 0, 0)
-        v_wq_quant(1)
+        wq_regroup(s_copy, 0)
+        wq_regroup(v_copy, 1)
+        wq_regroup(g_copy, 3)
         v_qx1(0, 0)
-        v_wq_quant(0)
-        pe_tx2(0)
         wq_regroup(s_copy, 2)
-        v_wq_quant(2)
-        v_wq_quant(3)
+        for c in (1, 0, 3, 2):
+            v_wq_quant(c)
         pe_tx1(0, 1)
-        x1_exit(v_copy, 0, 1)
-        pe_mt(0)
+        pe_tx2(0)
         x2_exit(s_copy, 0)
-        pe_pa(0)
-        mtx(v_copy, 0)
-        v_qx1(0, 1)
-        pe_tx1(1, 0)
-        x1_exit(v_copy, 1, 0)
+        x1_exit(s_copy, 0, 1)
+        pe_mt(0)
         pe_mt(1)
+        mtx(v_copy, 0)
+        pe_pa(0)
+        v_qx1(0, 1)
         pe_pb(0)
-        v_qx1(1, 0)
-        wv_regroup(s_copy, 0)
         mtx(v_copy, 1)
-        pe_mt(2)
-        pe_pa(1)
         s_th(0)
-        pe_tx2(1)
+        pe_pa(1)
         pe_pb(1)
-        mtx(s_copy, 2)
-        pe_mt(3)
-        pe_mt(5)
+        pe_mt(2)
+        pe_tx1(1, 0)
+        mtx(v_copy, 2)
+        pe_tx2(1)
+        x1_exit(v_copy, 1, 0)
         x2_exit(v_copy, 1)
-        s_ex(0)
-        s_th(1)
-        pe_pa(2)
-        pe_pb(2)
-        s_ex(1)
-        mtx(v_copy, 3)
-        pe_tx1(1, 1)
-        s_th(2)
-        mtx(v_copy, 5)
-        v_rinv(0)
-        pe_pa(3)
-        pe_mt(4)
-        norm("v", 0)
-        v_rinv(1)
-        norm("v", 1)
-        pe_pb(3)
-        x1_exit(v_copy, 1, 1)
-        pe_at(0)
-        v_qx1(1, 1)
-        s_ex(2)
-        mtx(s_copy, 4)
-        pe_at(1)
-        pe_pa(4)
-        pe_pb(4)
-        pe_mt(6)
-        s_th(3)
-        pe_pa(5)
-        v_rinv(2)
-        s_ex(3)
-        norm("v", 2)
-        wv_regroup(v_copy, 1)
-        atx(v_copy, 0)
-        v_rinv(3)
-        pe_mt(7)
-        pe_at(2)
-        s_th(4)
-        pe_pb(5)
-        atx(v_copy, 1)
-        mtx(s_copy, 6)
-        pe_pa(6)
-        s_ex(4)
-        s_th(5)
-        norm("v", 3)
-        v_wv_quant()
-        s_ex(5)
-        pe_at(3)
-        pe_pb(6)
-        s_th(6)
-        mtx(v_copy, 7)
-        v_qa(1)
-        s_ex(6)
-        v_rinv(4)
-        atx(v_copy, 3)
-        pe_pa(7)
-        atx(v_copy, 2)
-        v_rinv(5)
-        v_qa(0)
-        pe_pb(7)
-        norm("v", 5)
-        s_th(7)
-        norm("v", 4)
-        v_qa(3)
-        pe_at(5)
+        v_qx1(1, 0)
+        wv_regroup(g_copy, 0)
+        wv_regroup(g_copy, 1)
+
+        def atx_of(k):
+            atx(s_copy if k <= 3 or k >= 5 else v_copy, k)
+
+        for r in range(NK - 1):
+            s_th(r + 1)
+            s_ex(r)
+            if r + 3 < NK:
+                pe_mt(r + 3)
+            if r + 2 < NK:
+                pe_pa(r + 2)
+                pe_pb(r + 2)
+            if r == 0:
+                pe_tx1(1, 1)
+            if r >= 1:
+                v_rinv(r - 1)
+            if 2 <= r:
+                atx_of(r - 2)
+            if r == 6:
+                pe_mx2(0)
+                pe_mx2(1)
+            if r >= 1:
+                norm("v", r - 1)
+                pe_at(r - 1)
+            if r + 3 < NK:
+                mtx(v_copy, r + 3)
+            if r >= 2:
+                v_qa(r - 2)
+            if r == 0:
+                x1_exit(v_copy, 1, 1)
+            if r == 1:
+                v_qx1(1, 1)
+            if r == 4:
+                v_wv_quant()
         s_ex(7)
-        v_qa(2)
         v_rinv(6)
-        pe_at(4)
-        pe_mx2(0)
-        atx(v_copy, 5)
-        norm("s", 6)
-        v_rinv(7)
         v_y(0)
-        norm("s", 7)
-        atx(v_copy, 4)
-        pe_mx2(1)
-        s_sq(0)
+        norm("v", 6)
         pe_at(6)
-        v_qa(5)
-        v_y(1)
-        pe_at(7)
-        atx(s_copy, 6)
-        g_rs(0)
-        s_sq(1)
-        v_qa(4)
-        atx(v_copy, 7)
         pe_mx2(2)
-        v_qa(6)
-        g_rs(1)
-        v_y(2)
-        v_qa(7)
+        atx_of(5)
+        v_rinv(7)
+        v_y(1)
+        norm("v", 7)
+        pe_at(7)
         pe_mx2(3)
+        s_sq(0)
+        g_rs(0)
+        scale("g", 0)
+        v_qa(5)
+        v_y(2)
+        atx_of(6)
+        s_sq(1)
+        g_rs(1)
+        scale("g", 1)
+        atx_of(7)
+        v_qa(6)
+        v_qa(7)
         v_y(3)
-        scale("v", 1)
-        scale("s", 0)
-        s_sq(2)
         pe_mx2(4)
-        g_rs(2)
         pe_mx2(5)
+        s_sq(2)
+        g_rs(2)
+        scale("g", 2)
         s_sq(3)
-        v_y(4)
-        pe_ot(0, 1)
         g_rs(3)
-        s_sq(4)
-        g_rs(4)
-        v_y(5)
-        pe_mx2(6)
-        scale("v", 2)
-        ox(v_copy, 0, 1)
-        d_store(0, 1)
-        scale("v", 3)
+        scale("g", 3)
         pe_ot(0, 0)
-        v_y(6)
-        pe_mx2(7)
-        s_sq(5)
+        pe_ot(0, 1)
         ox(s_copy, 0, 0)
         d_store(0, 0)
-        s_sq(6)
-        v_y(7)
-        pe_ot(1, 0)
+        v_y(4)
+        pe_mx2(6)
+        v_y(5)
+        pe_mx2(7)
+        s_sq(4)
+        g_rs(4)
+        v_y(6)
+        s_sq(5)
         g_rs(5)
-        s_sq(7)
-        scale("v", 4)
-        ox(v_copy, 1, 0)
-        d_store(1, 0)
-        pe_ot(1, 1)
-        ox(s_copy, 1, 1)
-        d_store(1, 1)
+        v_y(7)
+        s_sq(6)
         g_rs(6)
+        s_sq(7)
         g_rs(7)
+        ox(v_copy, 0, 1)
+        d_store(0, 1)
+        pe_ot(1, 0)
+        pe_ot(1, 1)
+        scale("v", 4)
         scale("v", 5)
         pe_ot(2, 0)
-        ox(v_copy, 2, 0)
-        d_store(2, 0)
-        scale("s", 6)
-        scale("v", 7)
         pe_ot(2, 1)
-        ox(s_copy, 2, 1)
-        d_store(2, 1)
+        ox(v_copy, 1, 1)
+        d_store(1, 1)
+        ox(s_copy, 1, 0)
+        d_store(1, 0)
+        scale("v", 6)
+        scale("v", 7)
         pe_ot(3, 0)
         pe_ot(3, 1)
-        ox(s_copy, 3, 1)
-        d_store(3, 1)
-        ox(v_copy, 3, 0)
+        ox(s_copy, 2, 0)
+        d_store(2, 0)
+        ox(v_copy, 2, 1)
+        d_store(2, 1)
+        ox(s_copy, 3, 0)
         d_store(3, 0)
+        ox(v_copy, 3, 1)
+        d_store(3, 1)

@@ -34,7 +34,7 @@ def tile_attentionlayer_pa_kernel(tc, x1, x2, W_query, W_key, W_value, out):
         make_identity(nc, ident_f[:])
         neg_one = keep.tile([P, 1], F32, name="neg_one")
         nc.vector.memset(neg_one[:], -1.0)
-        neg_half = keep.tile([P, 1], F32, name="neg_half")
+        neg_half = keep.tile([P, 2], F32, name="neg_half")
         nc.vector.memset(neg_half[:], -0.5)
 
         x1n = [keep.tile([P, NI, T], BF16, name="x1n%d" % b) for b in range(B)]
@@ -237,7 +237,10 @@ def tile_attentionlayer_pa_kernel(tc, x1, x2, W_query, W_key, W_value, out):
         def pe_mx2(j):
             b, c = divmod(j, 4)
             cols = slice(P * c, P * c + P)
-            g_t[j] = psum.tile([P, S], F32, name="acc", tag="acc", bufs=ACC_BUFS)
+            if j % 2 == 0:
+                g_t[j] = psum.tile([P, S], F32, name="acc", tag="acc", bufs=ACC_BUFS)
+            else:
+                g_t[j] = psum.tile([P, S], F32, name="sp", tag="sp", bufs=SP_BUFS)
             nc.tensor.matmul_mx(
                 out=g_t[j][:],
                 lhsT=wvc[:, cols].bitcast(FP8X4),
@@ -256,18 +259,23 @@ def tile_attentionlayer_pa_kernel(tc, x1, x2, W_query, W_key, W_value, out):
 
         def s_sq(j):
             junk = work.tile([P, S], BF16, name="junk", bufs=2)
-            q_t[j] = small.tile([P, 1], F32, name="q")
-            nc.scalar.activation(out=junk[:], in_=y_t[j][:], func=ACT.Square, accum_out=q_t[j][:])
+            if j % 2 == 0:
+                q_t[j // 2] = small.tile([P, 2], F32, name="q")
+            col = j % 2
+            nc.scalar.activation(
+                out=junk[:], in_=y_t[j][:], func=ACT.Square, accum_out=q_t[j // 2][:, col : col + 1]
+            )
 
-        def g_rs(j):
-            qm = small.tile([P, 1], F32, name="qm")
-            nc.gpsimd.tensor_scalar(out=qm[:], in0=q_t[j][:], scalar1=EPS, scalar2=None, op0=ALU.max)
-            rs_t[j] = small.tile([P, 1], F32, name="rs")
-            nc.gpsimd.tensor_tensor(out=rs_t[j][:], in0=qm[:], in1=neg_half[:], op=ALU.pow)
+        def g_rs(r):
+            qm = small.tile([P, 2], F32, name="qm")
+            nc.gpsimd.tensor_scalar(out=qm[:], in0=q_t[r][:], scalar1=EPS, scalar2=None, op0=ALU.max)
+            rs_t[r] = small.tile([P, 2], F32, name="rs")
+            nc.gpsimd.tensor_tensor(out=rs_t[r][:], in0=qm[:], in1=neg_half[:], op=ALU.pow)
 
         def scale(eng, j):
             ys_t[j] = work.tile([P, S], F32, name="ys", bufs=8)
-            scale_rows(eng, ys_t[j][:], y_t[j][:], rs_t[j][:])
+            col = j % 2
+            scale_rows(eng, ys_t[j][:], y_t[j][:], rs_t[j // 2][:, col : col + 1])
 
         def pe_ot(r, h):
             ot_t[(r, h)] = psum.tile([P, 4, P], F32, name="ot", tag="tr", bufs=TR_BUFS)
@@ -318,15 +326,13 @@ def tile_attentionlayer_pa_kernel(tc, x1, x2, W_query, W_key, W_value, out):
         pe_pb(0)
         mtx(v_copy, 1)
         s_th(0)
+        pe_mt(2)
         pe_pa(1)
         pe_pb(1)
-        pe_mt(2)
         pe_tx1(1, 0)
         mtx(v_copy, 2)
         pe_tx2(1)
         x1_exit(v_copy, 1, 0)
-        x2_exit(v_copy, 1)
-        v_qx1(1, 0)
         wv_regroup(g_copy, 0)
         wv_regroup(g_copy, 1)
 
@@ -336,6 +342,8 @@ def tile_attentionlayer_pa_kernel(tc, x1, x2, W_query, W_key, W_value, out):
         for r in range(NK - 1):
             s_th(r + 1)
             s_ex(r)
+            if r == 0:
+                x2_exit(s_copy, 1)
             if r + 3 < NK:
                 pe_mt(r + 3)
             if r + 2 < NK:
@@ -358,6 +366,7 @@ def tile_attentionlayer_pa_kernel(tc, x1, x2, W_query, W_key, W_value, out):
             if r >= 2:
                 v_qa(r - 2)
             if r == 0:
+                v_qx1(1, 0)
                 x1_exit(v_copy, 1, 1)
             if r == 1:
                 v_qx1(1, 1)
@@ -367,8 +376,8 @@ def tile_attentionlayer_pa_kernel(tc, x1, x2, W_query, W_key, W_value, out):
         v_rinv(6)
         v_y(0)
         norm("v", 6)
-        pe_at(6)
         pe_mx2(2)
+        pe_at(6)
         atx_of(5)
         v_rinv(7)
         v_y(1)
@@ -376,48 +385,44 @@ def tile_attentionlayer_pa_kernel(tc, x1, x2, W_query, W_key, W_value, out):
         pe_at(7)
         pe_mx2(3)
         s_sq(0)
-        g_rs(0)
-        scale("g", 0)
         v_qa(5)
         v_y(2)
         atx_of(6)
         s_sq(1)
-        g_rs(1)
-        scale("g", 1)
+        g_rs(0)
         atx_of(7)
         v_qa(6)
-        v_qa(7)
         v_y(3)
+        v_qa(7)
         pe_mx2(4)
         pe_mx2(5)
         s_sq(2)
-        g_rs(2)
-        scale("g", 2)
+        scale("v", 0)
+        scale("v", 1)
         s_sq(3)
-        g_rs(3)
-        scale("g", 3)
+        g_rs(1)
+        v_y(4)
         pe_ot(0, 0)
         pe_ot(0, 1)
         ox(s_copy, 0, 0)
         d_store(0, 0)
-        v_y(4)
-        pe_mx2(6)
         v_y(5)
+        pe_mx2(6)
         pe_mx2(7)
         s_sq(4)
-        g_rs(4)
         v_y(6)
         s_sq(5)
-        g_rs(5)
-        v_y(7)
-        s_sq(6)
-        g_rs(6)
-        s_sq(7)
-        g_rs(7)
-        ox(v_copy, 0, 1)
-        d_store(0, 1)
+        g_rs(2)
+        scale("v", 2)
+        scale("v", 3)
         pe_ot(1, 0)
         pe_ot(1, 1)
+        v_y(7)
+        s_sq(6)
+        s_sq(7)
+        g_rs(3)
+        ox(v_copy, 0, 1)
+        d_store(0, 1)
         scale("v", 4)
         scale("v", 5)
         pe_ot(2, 0)

@@ -52,12 +52,12 @@ def tile_attentionlayer_pa_kernel(tc, x1, x2, W_query, W_key, W_value, out):
         nc.sync.dma_start(out=x1n[0][:, 2:4, :], in_=x1v[0][:, 2:4, :])
         nc.sync.dma_start(out=x2n[0][:], in_=x2v[0])
         nc.sync.dma_start(out=wk[:], in_=W_key.rearrange("(q e) c -> q e c", e=2))
-        nc.sync.dma_start(out=x1n[1][:], in_=x1v[1])
-        nc.sync.dma_start(out=x2n[1][:], in_=x2v[1])
         nc.sync.dma_start(
             out=wvr[:].rearrange("q (u e) c -> q u e c", u=2),
             in_=W_value.rearrange("(u q e) c -> q u e c", u=2, e=2),
         )
+        nc.sync.dma_start(out=x1n[1][:], in_=x1v[1])
+        nc.sync.dma_start(out=x2n[1][:], in_=x2v[1])
 
         x1g = [keep.tile([P, 4 * S], BF16, name="x1g%d" % b, align_bytes=64) for b in range(B)]
         x1c = [keep.tile([P, S], U32, name="x1c%d" % b, align_bytes=64) for b in range(B)]
@@ -118,6 +118,16 @@ def tile_attentionlayer_pa_kernel(tc, x1, x2, W_query, W_key, W_value, out):
             eng_copy(
                 out=wqg[:, 512 * c : 512 * c + 512].rearrange("p (c i t) -> p c t i", i=4, t=4),
                 in_=wqr[:, :, P * c : P * c + P].rearrange("p t (c i) -> p c t i", i=4),
+            )
+
+        def g_wq_regroup(c):
+            nc.gpsimd.tensor_scalar(
+                out=wqg[:, 512 * c : 512 * c + 512].rearrange("p (c t) -> p c t", t=4),
+                in0=wqr[:, :, P * c : P * c + P].rearrange("p t c -> p c t"),
+                scalar1=1.0,
+                scalar2=0.0,
+                op0=ALU.mult,
+                op1=ALU.add,
             )
 
         def v_wq_quant(c):
@@ -213,25 +223,30 @@ def tile_attentionlayer_pa_kernel(tc, x1, x2, W_query, W_key, W_value, out):
             scale_rows(eng, a_t[k][:], ex_t[k][:], ri_t[k][:])
 
         def pe_at(k):
-            at_t[k] = psum.tile([P, 2, P], F32, name="at", tag="tr", bufs=TR_BUFS)
+            if k % 2 == 0:
+                at_t[k // 2] = psum.tile([P, 2, 2, P], F32, name="at", tag="tr", bufs=TR_BUFS)
             a_words = a_t[k][:].bitcast(F32)
             for u in range(2):
-                nc.tensor.transpose(at_t[k][:, u, :], a_words[:, P * u : P * u + P], ident_f[:])
+                nc.tensor.transpose(
+                    at_t[k // 2][:, k % 2, u, :], a_words[:, P * u : P * u + P], ident_f[:]
+                )
 
-        def atx(eng_copy, k):
-            b, i = divmod(k, NI)
+        def atx(eng_copy, q):
+            b, h = divmod(q, 2)
             eng_copy(
-                out=ag[b][:].bitcast(F32)[:, 256 * i : 256 * i + 256].rearrange("p (s u) -> p s u", u=2),
-                in_=at_t[k][:].rearrange("p u s -> p s u"),
+                out=ag[b][:].bitcast(F32)[:, 512 * h : 512 * h + 512].rearrange(
+                    "p (i s u) -> p i s u", i=2, u=2
+                ),
+                in_=at_t[q][:].rearrange("p i u s -> p i s u"),
             )
 
-        def v_qa(k):
-            b, i = divmod(k, NI)
-            cols = slice(P * i, P * i + P)
+        def v_qa(q):
+            b, h = divmod(q, 2)
+            cols = slice(256 * h, 256 * h + 256)
             nc.vector.quantize_mx(
                 out=ac[b][:, cols].bitcast(FP8X4),
                 scales=asc[b][:, cols],
-                in_=ag[b][:, 512 * i : 512 * i + 512],
+                in_=ag[b][:, 1024 * h : 1024 * h + 1024],
             )
 
         def pe_mx2(j):
@@ -309,7 +324,7 @@ def tile_attentionlayer_pa_kernel(tc, x1, x2, W_query, W_key, W_value, out):
         x1_exit(v_copy, 0, 0)
         wq_regroup(s_copy, 0)
         wq_regroup(v_copy, 1)
-        wq_regroup(g_copy, 3)
+        g_wq_regroup(3)
         v_qx1(0, 0)
         wq_regroup(s_copy, 2)
         for c in (1, 0, 3, 2):
@@ -326,111 +341,143 @@ def tile_attentionlayer_pa_kernel(tc, x1, x2, W_query, W_key, W_value, out):
         pe_pb(0)
         mtx(v_copy, 1)
         s_th(0)
-        pe_mt(2)
         pe_pa(1)
+        pe_mt(2)
         pe_pb(1)
-        pe_tx1(1, 0)
         mtx(v_copy, 2)
-        pe_tx2(1)
-        x1_exit(v_copy, 1, 0)
         wv_regroup(g_copy, 0)
         wv_regroup(g_copy, 1)
+        s_th(1)
+        s_ex(0)
+        pe_mt(3)
+        pe_pa(2)
+        pe_pb(2)
+        mtx(v_copy, 3)
+        pe_tx1(1, 0)
+        pe_tx2(1)
+        v_wv_quant()
+        x1_exit(v_copy, 1, 0)
 
-        def atx_of(k):
-            atx(s_copy if k <= 3 or k >= 5 else v_copy, k)
+        s_ex(1)
+        s_th(2)
+        x2_exit(s_copy, 1)
+        v_rinv(0)
+        norm("g", 0)
+        pe_pa(3)
+        pe_pb(3)
+        pe_tx1(1, 1)
+        v_qx1(1, 0)
+        v_rinv(1)
+        norm("g", 1)
+        pe_mt(4)
+        mtx(v_copy, 4)
 
-        for r in range(NK - 1):
-            s_th(r + 1)
-            s_ex(r)
-            if r == 0:
-                x2_exit(s_copy, 1)
-            if r + 3 < NK:
-                pe_mt(r + 3)
-            if r + 2 < NK:
-                pe_pa(r + 2)
-                pe_pb(r + 2)
-            if r == 0:
-                pe_tx1(1, 1)
-            if r >= 1:
-                v_rinv(r - 1)
-            if 2 <= r:
-                atx_of(r - 2)
-            if r == 6:
-                pe_mx2(0)
-                pe_mx2(1)
-            if r >= 1:
-                norm("v", r - 1)
-                pe_at(r - 1)
-            if r + 3 < NK:
-                mtx(v_copy, r + 3)
-            if r >= 2:
-                v_qa(r - 2)
-            if r == 0:
-                v_qx1(1, 0)
-                x1_exit(v_copy, 1, 1)
-            if r == 1:
-                v_qx1(1, 1)
-            if r == 4:
-                v_wv_quant()
-        s_ex(7)
-        v_rinv(6)
+        s_th(3)
+        s_ex(2)
+        x1_exit(s_copy, 1, 1)
+        s_ex(3)
+        pe_mt(5)
+        pe_pa(4)
+        pe_at(0)
+        pe_pb(4)
+        pe_at(1)
+        v_rinv(2)
+        norm("g", 2)
+        mtx(v_copy, 5)
+        v_qx1(1, 1)
+
+        s_th(4)
+        atx(s_copy, 0)
+        pe_pa(5)
+        v_rinv(3)
+        norm("g", 3)
+        pe_mt(6)
+        pe_pb(5)
+        pe_at(2)
+        mtx(v_copy, 6)
+        v_qa(0)
+
+        s_th(5)
+        s_ex(4)
+        pe_mt(7)
+        pe_at(3)
+        pe_pa(6)
+        mtx(v_copy, 7)
+        atx(v_copy, 1)
+        pe_pb(6)
+        v_rinv(4)
+        norm("g", 4)
+
+        s_ex(5)
+        v_qa(1)
+        pe_pa(7)
+        pe_pb(7)
+        pe_mx2(0)
+        s_th(6)
+        s_ex(6)
+        v_rinv(5)
+        norm("v", 5)
+        pe_mx2(1)
+        pe_at(4)
+        pe_at(5)
         v_y(0)
-        norm("v", 6)
-        pe_mx2(2)
-        pe_at(6)
-        atx_of(5)
-        v_rinv(7)
+        s_th(7)
+        s_ex(7)
         v_y(1)
+        v_rinv(6)
+        atx(v_copy, 2)
+        pe_mx2(2)
+        v_rinv(7)
+        norm("v", 6)
+        pe_at(6)
         norm("v", 7)
         pe_at(7)
         pe_mx2(3)
         s_sq(0)
-        v_qa(5)
         v_y(2)
-        atx_of(6)
         s_sq(1)
         g_rs(0)
-        atx_of(7)
-        v_qa(6)
+        v_qa(2)
+        atx(s_copy, 3)
         v_y(3)
-        v_qa(7)
+        v_qa(3)
         pe_mx2(4)
         pe_mx2(5)
         s_sq(2)
-        scale("v", 0)
         scale("v", 1)
         s_sq(3)
+        scale("s", 0)
         g_rs(1)
+        scale("g", 2)
         v_y(4)
-        pe_ot(0, 0)
-        pe_ot(0, 1)
-        ox(s_copy, 0, 0)
-        d_store(0, 0)
         v_y(5)
         pe_mx2(6)
+        pe_ot(0, 0)
+        pe_ot(0, 1)
         pe_mx2(7)
         s_sq(4)
         v_y(6)
         s_sq(5)
         g_rs(2)
-        scale("v", 2)
-        scale("v", 3)
-        pe_ot(1, 0)
-        pe_ot(1, 1)
+        ox(s_copy, 0, 0)
+        d_store(0, 0)
         v_y(7)
         s_sq(6)
         s_sq(7)
         g_rs(3)
+        scale("v", 3)
+        pe_ot(1, 1)
+        pe_ot(1, 0)
         ox(v_copy, 0, 1)
         d_store(0, 1)
         scale("v", 4)
         scale("v", 5)
         pe_ot(2, 0)
         pe_ot(2, 1)
-        ox(v_copy, 1, 1)
-        d_store(1, 1)
         ox(s_copy, 1, 0)
         d_store(1, 0)
+        ox(v_copy, 1, 1)
+        d_store(1, 1)
         scale("v", 6)
         scale("v", 7)
         pe_ot(3, 0)

from contextlib import ExitStack

import concourse.mybir as mybir
from concourse.masks import make_identity

F32 = mybir.dt.float32
BF16 = mybir.dt.bfloat16
U32 = mybir.dt.uint32
U8 = mybir.dt.uint8
FP8X4 = mybir.dt.float8_e4m3fn_x4
ACT = mybir.ActivationFunctionType
ALU = mybir.AluOpType

P = 128
B, S, T, U, F = 2, 512, 512, 512, 256
NI = S // P
EPS = 1e-12

FLOPS = 2 * B * S * T * U + 2 * B * S * F * U + 2 * B * S * U * T


TR_BUFS, ACC_BUFS, SP_BUFS = 4, 2, 2

def tile_attentionlayer_pa_kernel(tc, x1, x2, W_query, W_key, W_value, out):
    nc = tc.nc
    with ExitStack() as ctx:
        keep = ctx.enter_context(tc.tile_pool(name="keep", bufs=1))
        work = ctx.enter_context(tc.tile_pool(name="work", bufs=3))
        small = ctx.enter_context(tc.tile_pool(name="small", bufs=4))
        psum = ctx.enter_context(tc.psum_pool(name="psum", bufs=1))
        ctx.enter_context(tc.manual_schedule())

        ident_f = keep.tile([P, P], F32, name="ident_f")
        make_identity(nc, ident_f[:])
        neg_one = keep.tile([P, 1], F32, name="neg_one")
        nc.vector.memset(neg_one[:], -1.0)
        neg_half = keep.tile([P, 2], F32, name="neg_half")
        nc.vector.memset(neg_half[:], -0.5)

        x1n = [keep.tile([P, NI, T], BF16, name="x1n%d" % b) for b in range(B)]
        x2n = [keep.tile([P, NI, F], BF16, name="x2n%d" % b) for b in range(B)]
        wqr = keep.tile([P, 4, U], BF16, name="wqr")
        wk = keep.tile([P, 2, U], BF16, name="wk")
        wvr = keep.tile([P, 4, T], BF16, name="wvr")
        x1v = [x1[b].rearrange("(p i) t -> p i t", i=NI) for b in range(B)]
        x2v = [x2[b].rearrange("(p i) f -> p i f", i=NI) for b in range(B)]
        nc.sync.dma_start(out=x1n[0][:, 0:2, :], in_=x1v[0][:, 0:2, :])
        nc.sync.dma_start(
            out=wqr[:].rearrange("q (u e) c -> q u e c", u=2),
            in_=W_query.rearrange("(u q e) c -> q u e c", u=2, e=2),
        )
        nc.sync.dma_start(out=x1n[0][:, 2:4, :], in_=x1v[0][:, 2:4, :])
        nc.sync.dma_start(out=x2n[0][:], in_=x2v[0])
        nc.sync.dma_start(out=wk[:], in_=W_key.rearrange("(q e) c -> q e c", e=2))
        nc.sync.dma_start(
            out=wvr[:].rearrange("q (u e) c -> q u e c", u=2),
            in_=W_value.rearrange("(u q e) c -> q u e c", u=2, e=2),
        )
        nc.sync.dma_start(out=x1n[1][:], in_=x1v[1])
        nc.sync.dma_start(out=x2n[1][:], in_=x2v[1])

        x1g = [keep.tile([P, 4 * S], BF16, name="x1g%d" % b, align_bytes=64) for b in range(B)]
        x1c = [keep.tile([P, S], U32, name="x1c%d" % b, align_bytes=64) for b in range(B)]
        x1s = [keep.tile([P, S], U8, name="x1s%d" % b, align_bytes=64) for b in range(B)]
        x2t = [keep.tile([P, S], F32, name="x2t%d" % b) for b in range(B)]
        ag = [keep.tile([P, 4 * S], BF16, name="ag%d" % b, align_bytes=64) for b in range(B)]
        ac = [keep.tile([P, S], U32, name="ac%d" % b, align_bytes=64) for b in range(B)]
        asc = [keep.tile([P, S], U8, name="asc%d" % b, align_bytes=64) for b in range(B)]
        wqg = keep.tile([P, 4 * U], BF16, name="wqg", align_bytes=64)
        wqc = keep.tile([P, U], U32, name="wqc", align_bytes=64)
        wqs = keep.tile([P, U], U8, name="wqs", align_bytes=64)
        wvg = keep.tile([P, 4 * T], BF16, name="wvg", align_bytes=64)
        wvc = keep.tile([P, T], U32, name="wvc", align_bytes=64)
        wvs = keep.tile([P, T], U8, name="wvs", align_bytes=64)
        osb = {}
        for r in range(2 * B):
            for h in range(2):
                osb[(r, h)] = keep.tile([P, 2, 256], F32, name="osb%d%d" % (r, h))

        sm_t, sp_t, psb_t, sc_t, th_t, ex_t, ss_t, a_t, at_t = {}, {}, {}, {}, {}, {}, {}, {}, {}
        tin_t, g_t, y_t, q_t, rs_t, ys_t, ot_t, ri_t = {}, {}, {}, {}, {}, {}, {}, {}

        def pe_tx1(b, h):
            x1w = x1n[b][:].bitcast(F32)
            tin = psum.tile([P, 4, P], F32, name="tin", tag="tr", bufs=TR_BUFS)
            tin_t[("x1", b, h)] = tin
            for i2 in range(2):
                for u in range(2):
                    nc.tensor.transpose(
                        tin[:, 2 * i2 + u, :], x1w[:, 2 * h + i2, P * u : P * u + P], ident_f[:]
                    )

        def x1_exit(eng_copy, b, h):
            dst = x1g[b][:].bitcast(F32)[:, 512 * h : 512 * h + 512]
            eng_copy(
                out=dst.rearrange("p (i s u) -> p i s u", i=2, u=2),
                in_=tin_t[("x1", b, h)][:].rearrange("p (i u) s -> p i s u", u=2),
            )

        def v_qx1(b, h):
            nc.vector.quantize_mx(
                out=x1c[b][:, 256 * h : 256 * h + 256].bitcast(FP8X4),
                scales=x1s[b][:, 256 * h : 256 * h + 256],
                in_=x1g[b][:, 1024 * h : 1024 * h + 1024],
            )

        def pe_tx2(b):
            x2w = x2n[b][:].bitcast(F32)
            tin = psum.tile([P, 4, P], F32, name="tin", tag="tr", bufs=TR_BUFS)
            tin_t[("x2", b)] = tin
            for i in range(NI):
                nc.tensor.transpose(tin[:, i, :], x2w[:, i, :], ident_f[:])

        def x2_exit(eng_copy, b):
            eng_copy(out=x2t[b][:], in_=tin_t[("x2", b)][:].rearrange("p i s -> p (i s)"))

        def wq_regroup(eng_copy, c):
            eng_copy(
                out=wqg[:, 512 * c : 512 * c + 512].rearrange("p (c i t) -> p c t i", i=4, t=4),
                in_=wqr[:, :, P * c : P * c + P].rearrange("p t (c i) -> p c t i", i=4),
            )

        def g_wq_regroup(c):
            nc.gpsimd.tensor_scalar(
                out=wqg[:, 512 * c : 512 * c + 512].rearrange("p (c t) -> p c t", t=4),
                in0=wqr[:, :, P * c : P * c + P].rearrange("p t c -> p c t"),
                scalar1=1.0,
                scalar2=0.0,
                op0=ALU.mult,
                op1=ALU.add,
            )

        def v_wq_quant(c):
            cc = slice(P * c, P * c + P)
            nc.vector.quantize_mx(
                out=wqc[:, cc].bitcast(FP8X4), scales=wqs[:, cc], in_=wqg[:, 512 * c : 512 * c + 512]
            )

        def wv_regroup(eng_copy, u):
            eng_copy(
                out=wvg[:, 1024 * u : 1024 * u + 1024].rearrange("p (e q j) -> p e q j", e=2, j=4),
                in_=wvr[:, :, 256 * u : 256 * u + 256].rearrange("p j (q e) -> p e q j", e=2),
            )

        def v_wv_quant():
            nc.vector.quantize_mx(out=wvc[:].bitcast(FP8X4), scales=wvs[:], in_=wvg[:])

        def g_copy(out, in_):
            nc.gpsimd.tensor_scalar(out=out, in0=in_, scalar1=1.0, scalar2=0.0, op0=ALU.mult, op1=ALU.add)

        mt_ps, mt_sb = {}, {}

        def pe_mt(k):
            b, i = divmod(k, NI)
            cols = slice(P * i, P * i + P)
            mt_ps[k] = psum.tile([P, 4, P], F32, name="acc", tag="acc", bufs=ACC_BUFS)
            for c in range(4):
                cc = slice(P * c, P * c + P)
                nc.tensor.matmul_mx(
                    out=mt_ps[k][:, c, :],
                    lhsT=wqc[:, cc].bitcast(FP8X4),
                    lhsT_scale=wqs[:, cc],
                    rhs=x1c[b][:, cols].bitcast(FP8X4),
                    rhs_scale=x1s[b][:, cols],
                    start=True,
                    stop=True,
                )

        def mtx(eng_copy, k):
            mt_sb[k] = work.tile([P, 4, P], F32, name="mt", bufs=3)
            eng_copy(out=mt_sb[k][:], in_=mt_ps[k][:])

        def pe_pa(k):
            b, i = divmod(k, NI)
            cols = slice(P * i, P * i + P)
            sp = psum.tile([P, U], F32, name="sp", tag="sp", bufs=SP_BUFS)
            sc_t[k] = sp
            x2b = x2t[b][:].bitcast(BF16).rearrange("p (s e) -> p s e", e=2)
            for e in range(2):
                nc.tensor.matmul(
                    sp[:], lhsT=x2b[:, cols, e], rhs=wk[:, e, :], start=(e == 0), stop=False
                )

        def pe_pb(k):
            sp = sc_t[k]
            for c in range(4):
                nc.tensor.matmul(
                    sp[:, P * c : P * c + P],
                    lhsT=mt_sb[k][:, c, :],
                    rhs=ident_f[:],
                    is_transpose=True,
                    start=False,
                    stop=(c == 3),
                )

        def s_th(k):
            th_t[k] = work.tile([P, U], F32, name="th")
            nc.scalar.activation(out=th_t[k][:], in_=sc_t[k][:], func=ACT.Tanh)

        def s_ex(k):
            ex_t[k] = work.tile([P, U], F32, name="ex")
            ss_t[k] = small.tile([P, 1], F32, name="ssum")
            nc.scalar.activation(
                out=ex_t[k][:], in_=th_t[k][:], func=ACT.Exp, bias=neg_one[:], accum_out=ss_t[k][:]
            )

        def v_rinv(k):
            ri_t[k] = small.tile([P, 1], F32, name="rinv")
            nc.vector.reciprocal(out=ri_t[k][:], in_=ss_t[k][:])

        def scale_rows(eng, dst, src, col):
            if eng == "v":
                nc.vector.tensor_scalar(out=dst, in0=src, scalar1=col, scalar2=None, op0=ALU.mult)
            elif eng == "s":
                nc.scalar.activation(out=dst, in_=src, func=ACT.Copy, scale=col)
            else:
                nc.gpsimd.tensor_scalar(
                    out=dst, in0=src, scalar1=col, scalar2=0.0, op0=ALU.mult, op1=ALU.add
                )

        def norm(eng, k):
            a_t[k] = work.tile([P, U], BF16, name="a")
            scale_rows(eng, a_t[k][:], ex_t[k][:], ri_t[k][:])

        def pe_at(k):
            if k % 2 == 0:
                at_t[k // 2] = psum.tile([P, 2, 2, P], F32, name="at", tag="tr", bufs=TR_BUFS)
            a_words = a_t[k][:].bitcast(F32)
            for u in range(2):
                nc.tensor.transpose(
                    at_t[k // 2][:, k % 2, u, :], a_words[:, P * u : P * u + P], ident_f[:]
                )

        def atx(eng_copy, q):
            b, h = divmod(q, 2)
            eng_copy(
                out=ag[b][:].bitcast(F32)[:, 512 * h : 512 * h + 512].rearrange(
                    "p (i s u) -> p i s u", i=2, u=2
                ),
                in_=at_t[q][:].rearrange("p i u s -> p i s u"),
            )

        def v_qa(q):
            b, h = divmod(q, 2)
            cols = slice(256 * h, 256 * h + 256)
            nc.vector.quantize_mx(
                out=ac[b][:, cols].bitcast(FP8X4),
                scales=asc[b][:, cols],
                in_=ag[b][:, 1024 * h : 1024 * h + 1024],
            )

        def pe_mx2(j):
            b, c = divmod(j, 4)
            cols = slice(P * c, P * c + P)
            if j % 2 == 0:
                g_t[j] = psum.tile([P, S], F32, name="acc", tag="acc", bufs=ACC_BUFS)
            else:
                g_t[j] = psum.tile([P, S], F32, name="sp", tag="sp", bufs=SP_BUFS)
            nc.tensor.matmul_mx(
                out=g_t[j][:],
                lhsT=wvc[:, cols].bitcast(FP8X4),
                lhsT_scale=wvs[:, cols],
                rhs=ac[b][:].bitcast(FP8X4),
                rhs_scale=asc[b][:],
                start=True,
                stop=True,
            )

        def v_y(j):
            b, c = divmod(j, 4)
            y_t[j] = work.tile([P, S], F32, name="y", bufs=8)
            x1f = x1g[b][:].rearrange("p (s t) -> p s t", t=4)
            nc.vector.tensor_tensor(out=y_t[j][:], in0=g_t[j][:], in1=x1f[:, :, c], op=ALU.mult)

        def s_sq(j):
            junk = work.tile([P, S], BF16, name="junk", bufs=2)
            if j % 2 == 0:
                q_t[j // 2] = small.tile([P, 2], F32, name="q")
            col = j % 2
            nc.scalar.activation(
                out=junk[:], in_=y_t[j][:], func=ACT.Square, accum_out=q_t[j // 2][:, col : col + 1]
            )

        def g_rs(r):
            qm = small.tile([P, 2], F32, name="qm")
            nc.gpsimd.tensor_scalar(out=qm[:], in0=q_t[r][:], scalar1=EPS, scalar2=None, op0=ALU.max)
            rs_t[r] = small.tile([P, 2], F32, name="rs")
            nc.gpsimd.tensor_tensor(out=rs_t[r][:], in0=qm[:], in1=neg_half[:], op=ALU.pow)

        def scale(eng, j):
            ys_t[j] = work.tile([P, S], F32, name="ys", bufs=8)
            col = j % 2
            scale_rows(eng, ys_t[j][:], y_t[j][:], rs_t[j // 2][:, col : col + 1])

        def pe_ot(r, h):
            ot_t[(r, h)] = psum.tile([P, 4, P], F32, name="ot", tag="tr", bufs=TR_BUFS)
            for i2 in range(2):
                for e in range(2):
                    si = P * (2 * h + i2)
                    nc.tensor.transpose(
                        ot_t[(r, h)][:, 2 * i2 + e, :], ys_t[2 * r + e][:, si : si + P], ident_f[:]
                    )

        def ox(eng_copy, r, h):
            eng_copy(
                out=osb[(r, h)][:].rearrange("p i (q e) -> p i q e", e=2),
                in_=ot_t[(r, h)][:].rearrange("p (i e) q -> p i q e", e=2),
            )

        def d_store(r, h):
            b, u = divmod(r, 2)
            nc.sync.dma_start(
                out=out[b].rearrange("(p i) t -> p i t", i=NI)[
                    :, 2 * h : 2 * h + 2, 256 * u : 256 * u + 256
                ],
                in_=osb[(r, h)][:],
            )

        s_copy = nc.scalar.copy
        v_copy = nc.vector.tensor_copy
        NK = B * NI

        pe_tx1(0, 0)
        x1_exit(v_copy, 0, 0)
        wq_regroup(s_copy, 0)
        wq_regroup(v_copy, 1)
        g_wq_regroup(3)
        v_qx1(0, 0)
        wq_regroup(s_copy, 2)
        for c in (1, 0, 3, 2):
            v_wq_quant(c)
        pe_tx1(0, 1)
        pe_tx2(0)
        x2_exit(s_copy, 0)
        x1_exit(s_copy, 0, 1)
        pe_mt(0)
        pe_mt(1)
        mtx(v_copy, 0)
        pe_pa(0)
        v_qx1(0, 1)
        pe_pb(0)
        mtx(v_copy, 1)
        s_th(0)
        pe_pa(1)
        pe_mt(2)
        pe_pb(1)
        mtx(v_copy, 2)
        wv_regroup(g_copy, 0)
        wv_regroup(g_copy, 1)
        s_th(1)
        s_ex(0)
        pe_mt(3)
        pe_pa(2)
        pe_pb(2)
        mtx(v_copy, 3)
        pe_tx1(1, 0)
        pe_tx2(1)
        v_wv_quant()
        x1_exit(v_copy, 1, 0)

        s_ex(1)
        s_th(2)
        x2_exit(s_copy, 1)
        v_rinv(0)
        norm("g", 0)
        pe_pa(3)
        pe_pb(3)
        pe_tx1(1, 1)
        v_qx1(1, 0)
        v_rinv(1)
        norm("g", 1)
        pe_mt(4)
        mtx(v_copy, 4)

        s_th(3)
        s_ex(2)
        x1_exit(s_copy, 1, 1)
        s_ex(3)
        pe_mt(5)
        pe_pa(4)
        pe_at(0)
        pe_pb(4)
        pe_at(1)
        v_rinv(2)
        norm("g", 2)
        mtx(v_copy, 5)
        v_qx1(1, 1)

        s_th(4)
        atx(s_copy, 0)
        pe_pa(5)
        v_rinv(3)
        norm("g", 3)
        pe_mt(6)
        pe_pb(5)
        pe_at(2)
        mtx(v_copy, 6)
        v_qa(0)

        s_th(5)
        s_ex(4)
        pe_mt(7)
        pe_at(3)
        pe_pa(6)
        mtx(v_copy, 7)
        atx(v_copy, 1)
        pe_pb(6)
        v_rinv(4)
        norm("g", 4)

        s_ex(5)
        v_qa(1)
        pe_pa(7)
        pe_pb(7)
        pe_mx2(0)
        s_th(6)
        s_ex(6)
        v_rinv(5)
        norm("v", 5)
        pe_mx2(1)
        pe_at(4)
        pe_at(5)
        v_y(0)
        s_th(7)
        s_ex(7)
        v_y(1)
        v_rinv(6)
        atx(v_copy, 2)
        pe_mx2(2)
        v_rinv(7)
        norm("v", 6)
        pe_at(6)
        norm("v", 7)
        pe_at(7)
        pe_mx2(3)
        s_sq(0)
        v_y(2)
        s_sq(1)
        g_rs(0)
        v_qa(2)
        atx(s_copy, 3)
        v_y(3)
        v_qa(3)
        pe_mx2(4)
        pe_mx2(5)
        s_sq(2)
        scale("v", 1)
        s_sq(3)
        scale("s", 0)
        g_rs(1)
        scale("g", 2)
        v_y(4)
        v_y(5)
        pe_mx2(6)
        pe_ot(0, 0)
        pe_ot(0, 1)
        pe_mx2(7)
        s_sq(4)
        v_y(6)
        s_sq(5)
        g_rs(2)
        ox(s_copy, 0, 0)
        d_store(0, 0)
        v_y(7)
        s_sq(6)
        s_sq(7)
        g_rs(3)
        scale("v", 3)
        pe_ot(1, 1)
        pe_ot(1, 0)
        ox(v_copy, 0, 1)
        d_store(0, 1)
        scale("v", 4)
        scale("v", 5)
        pe_ot(2, 0)
        pe_ot(2, 1)
        ox(s_copy, 1, 0)
        d_store(1, 0)
        ox(v_copy, 1, 1)
        d_store(1, 1)
        scale("v", 6)
        scale("v", 7)
        pe_ot(3, 0)
        pe_ot(3, 1)
        ox(s_copy, 2, 0)
        d_store(2, 0)
        ox(v_copy, 2, 1)
        d_store(2, 1)
        ox(s_copy, 3, 0)
        d_store(3, 0)
        ox(v_copy, 3, 1)
        d_store(3, 1)
